import numpy as np
import ml_dtypes


def mxq(x, axis, fmt="e4m3"):
    dtype, down = {"e4m3": (ml_dtypes.float8_e4m3fn, 7), "e5m2": (ml_dtypes.float8_e5m2, 14)}[fmt]
    v = np.moveaxis(np.asarray(x, np.float32).astype(ml_dtypes.bfloat16).astype(np.float64), axis, -1)
    blocks = v.reshape(v.shape[:-1] + (-1, 32))
    amax = np.abs(blocks).max(-1, keepdims=True)
    byte = np.maximum(np.where(amax > 0, np.frexp(amax)[1] - 1 + 127, 0) - down, 1)
    scale = np.exp2(byte - 127.0)
    codes = (blocks / scale).astype(np.float32).astype(dtype).astype(np.float64)
    return np.moveaxis((codes * scale).reshape(v.shape), -1, axis)


WIDE = False


def mx_kscale(k):
    if not WIDE:
        return np.ones(k)
    levels = np.array([10, -10, 5, -5, 0])
    a = np.random.permutation(np.resize(levels, k // 512 * 4)).reshape(k // 512, 4)
    idx = np.arange(k)
    return np.exp2(a[idx // 512, idx % 128 // 32])


BF16 = ml_dtypes.bfloat16


def bf(x):
    return np.asarray(x, np.float32).astype(BF16)


def f64(x):
    return np.asarray(x).astype(np.float64)


B, T, D = 4, 32, 2048


def sigmoid(v):
    return 1.0 / (1.0 + np.exp(-v))


def setup_inputs():
    s = mx_kscale(D)
    t = np.exp2(np.round(np.log2(mx_kscale(D)) / 2))
    w = 1.2 / np.sqrt(D)
    wo = 1.6 / np.sqrt(D)
    return {"x": bf(np.random.standard_normal((B, T, D)) * s),
            "state": bf(np.random.standard_normal((B, T, D)) * t),
            "Wk": bf(np.random.standard_normal((D, D)) * w / s[None, :]),
            "Wv": bf(np.random.standard_normal((D, D)) * w / s[None, :] * t[:, None]),
            "Wr": bf(np.random.standard_normal((D, D)) * w / s[None, :]),
            "Wo": bf(np.random.standard_normal((D, D)) * wo / t[None, :]),
            "time_decay": bf(np.random.uniform(-3.0, 1.0, D)),
            "time_curve": bf(np.random.uniform(0.0, 1.0, D))}


def reference(x, state, Wk, Wv, Wr, Wo, time_decay, time_curve):
    x = f64(x)
    tc = f64(time_curve)
    xx = np.concatenate([np.zeros_like(x[:, :1]), x[:, :-1]], axis=1)
    xm = x * tc + xx * (1.0 - tc)
    xq = mxq(xm, 2, "e4m3")
    k = xq @ mxq(f64(Wk), 1, "e4m3").T
    v = xq @ mxq(f64(Wv), 1, "e4m3").T
    r = xq @ mxq(f64(Wr), 1, "e4m3").T
    sr = sigmoid(r)
    decay = np.exp(-np.exp(f64(time_decay)))
    new_state = k * v + decay * f64(state)
    out = mxq(sr * new_state, 2, "e4m3") @ mxq(f64(Wo), 1, "e4m3").T
    return out, new_state

@@ -1,0 +1,269 @@
+from contextlib import ExitStack
+
+import concourse.mybir as mybir
+from concourse.masks import make_identity
+
+F32 = mybir.dt.float32
+BF16 = mybir.dt.bfloat16
+U32 = mybir.dt.uint32
+U8 = mybir.dt.uint8
+FP8X4 = mybir.dt.float8_e4m3fn_x4
+MULT = mybir.AluOpType.mult
+ADD = mybir.AluOpType.add
+ACT = mybir.ActivationFunctionType
+
+P = 128
+TOKENS = 128
+SEQ_LEN = 32
+CHANNELS = 2048
+PACK = 4
+PAIR = 2
+PASSES = CHANNELS // (P * PACK)
+UNITS = CHANNELS // (P * PAIR)
+ROW_WORDS = CHANNELS // PAIR
+BANK = 512
+BANK_BLOCKS = BANK // P
+CHUNK_BANKS = ROW_WORDS // BANK
+LOAD_AHEAD = 6
+RAW_BUFS = 12
+
+FLOPS = 4 * 2 * TOKENS * CHANNELS * CHANNELS
+
+
+def tile_rwkvtimemix_pa_kernel(tc, x, state, Wk, Wv, Wr, Wo, time_decay, time_curve, out_0, out_1):
+    nc = tc.nc
+    weights = (Wk, Wv, Wr, Wo)
+    out_rows = out_0.rearrange("b t d -> (b t) d")
+    new_state_rows = out_1.rearrange("b t d -> (b t) d")
+
+    rounds = []
+    for j in range(UNITS):
+        for e in range(PAIR):
+            rounds.append([(0, j, e), (1, j, e), (2, j, e)])
+    first_out_round = len(rounds)
+    for j in range(UNITS):
+        rounds.append([(3, j, 0), (3, j, 1)])
+
+    with ExitStack() as ctx:
+        ctx.enter_context(tc.manual_schedule())
+        keep = ctx.enter_context(tc.tile_pool(name="keep", bufs=1))
+        raw_pool = ctx.enter_context(tc.tile_pool(name="raw", bufs=RAW_BUFS))
+        grouped_pool = ctx.enter_context(tc.tile_pool(name="grouped", bufs=4))
+        codes_pool = ctx.enter_context(tc.tile_pool(name="codes", bufs=6))
+        work = ctx.enter_context(tc.tile_pool(name="work", bufs=2))
+        stores = ctx.enter_context(tc.tile_pool(name="stores", bufs=4))
+        banks = ctx.enter_context(tc.psum_pool(name="banks", bufs=6))
+        sums = ctx.enter_context(tc.psum_pool(name="sums", bufs=2))
+
+        vectors = keep.tile([P, P * PAIR], BF16)
+        nc.vector.memset(vectors[:], 0.0)
+        nc.sync.dma_start(out=vectors[0:UNITS, :], in_=time_curve.rearrange("(j c) -> j c", j=UNITS))
+        nc.sync.dma_start(out=vectors[UNITS : 2 * UNITS, :], in_=time_decay.rearrange("(j c) -> j c", j=UNITS))
+
+        ident = keep.tile([P, P], F32)
+        make_identity(nc, ident[:])
+        shift = keep.tile([P, P], F32)
+        nc.vector.memset(shift[:], 0.0)
+        nc.vector.tensor_copy(
+            out=shift[:].rearrange("p (b t) -> p b t", t=SEQ_LEN)[:, :, 1:SEQ_LEN],
+            in_=ident[:].rearrange("p (b t) -> p b t", t=SEQ_LEN)[:, :, 0 : SEQ_LEN - 1],
+        )
+
+        x_sb = keep.tile([P, CHANNELS], BF16)
+        nc.sync.dma_start(out=x_sb[:], in_=x.rearrange("b t d -> (b t) d"))
+        state_sb = keep.tile([P, CHANNELS], BF16)
+        nc.sync.dma_start(out=state_sb[:], in_=state.rearrange("b t d -> (b t) d"))
+
+        raw_words = {}
+
+        def load_round(r):
+            for w, j, e in rounds[r]:
+                if (w, j) not in raw_words:
+                    raw = raw_pool.tile([P, PAIR * CHANNELS], BF16)
+                    unit_rows = weights[w][j * P * PAIR : (j + 1) * P * PAIR, :]
+                    nc.sync.dma_start(out=raw[:], in_=unit_rows.rearrange("(p e) k -> p (e k)", e=PAIR))
+                    raw_words[(w, j)] = raw[:].bitcast(F32)
+
+        for r in range(LOAD_AHEAD):
+            load_round(r)
+
+        bank = banks.tile([P, BANK], F32, tag="bank")
+        nc.tensor.transpose(bank[:, 0:P], vectors[:].bitcast(F32), ident[:])
+        per_channel = keep.tile([P, 2 * UNITS * PAIR], F32)
+        nc.vector.tensor_copy(out=per_channel[:], in_=bank[:].bitcast(BF16)[:, 0 : 2 * UNITS * PAIR])
+        curve = per_channel[:, 0 : UNITS * PAIR]
+        one_minus_curve = keep.tile([P, UNITS * PAIR], F32)
+        nc.vector.tensor_scalar(out=one_minus_curve[:], in0=curve, scalar1=-1.0, scalar2=1.0, op0=MULT, op1=ADD)
+        exp_decay = keep.tile([P, UNITS * PAIR], F32)
+        nc.scalar.activation(out=exp_decay[:], in_=per_channel[:, UNITS * PAIR : 2 * UNITS * PAIR], func=ACT.Exp)
+        decay = keep.tile([P, UNITS * PAIR], F32)
+        nc.scalar.activation(out=decay[:], in_=exp_decay[:], func=ACT.Exp, scale=-1.0)
+
+        def over_tokens(columns, units):
+            pairs = columns.rearrange("p (j e) -> p j e", e=PAIR)[:, units, :]
+            return pairs.unsqueeze(2).to_broadcast([P, BANK_BLOCKS, TOKENS, PAIR])
+
+        x_words = x_sb[:].bitcast(F32)
+        now_part = keep.tile([P, UNITS, TOKENS, PAIR], F32)
+        before_part = keep.tile([P, UNITS, TOKENS, PAIR], F32)
+        xm_grouped = keep.tile([P, PASSES, TOKENS, PACK], BF16, align_bytes=64)
+        for half in range(UNITS // BANK_BLOCKS):
+            units = slice(half * BANK_BLOCKS, (half + 1) * BANK_BLOCKS)
+            now = banks.tile([P, BANK], F32, tag="bank")
+            before = banks.tile([P, BANK], F32, tag="bank")
+            for target, mover in ((now, ident), (before, shift)):
+                for q in range(BANK_BLOCKS):
+                    j = half * BANK_BLOCKS + q
+                    nc.tensor.transpose(target[:, q * P : (q + 1) * P], x_words[:, j * P : (j + 1) * P], mover[:])
+            nc.vector.tensor_tensor(
+                out=now_part[:, units, :, :],
+                in0=now[:].bitcast(BF16).rearrange("p (j k e) -> p j k e", j=BANK_BLOCKS, e=PAIR),
+                in1=over_tokens(curve, units),
+                op=MULT,
+            )
+            nc.vector.tensor_tensor(
+                out=before_part[:, units, :, :],
+                in0=before[:].bitcast(BF16).rearrange("p (j k e) -> p j k e", j=BANK_BLOCKS, e=PAIR),
+                in1=over_tokens(one_minus_curve[:], units),
+                op=MULT,
+            )
+            for g in range(half * BANK_BLOCKS // PAIR, (half + 1) * BANK_BLOCKS // PAIR):
+                nc.vector.tensor_tensor(
+                    out=xm_grouped[:, g, :, :].rearrange("p k (u e) -> p k u e", e=PAIR),
+                    in0=now_part[:, PAIR * g : PAIR * g + PAIR, :, :].rearrange("p u k e -> p k u e"),
+                    in1=before_part[:, PAIR * g : PAIR * g + PAIR, :, :].rearrange("p u k e -> p k u e"),
+                    op=ADD,
+                )
+        xm_codes = keep.tile([P, PASSES * TOKENS], U32, align_bytes=64)
+        xm_scales = keep.tile([P, PASSES * TOKENS], U8, align_bytes=64)
+        nc.vector.quantize_mx(
+            out=xm_codes[:].bitcast(FP8X4),
+            scales=xm_scales[:],
+            in_=xm_grouped[:].rearrange("p g k t -> p (g k t)"),
+        )
+
+        state_words = state_sb[:].bitcast(F32)
+        state_t = keep.tile([P, UNITS * TOKENS], F32)
+        for half in range(UNITS // BANK_BLOCKS):
+            bank = banks.tile([P, BANK], F32, tag="bank")
+            for q in range(BANK_BLOCKS):
+                j = half * BANK_BLOCKS + q
+                nc.tensor.transpose(bank[:, q * P : (q + 1) * P], state_words[:, j * P : (j + 1) * P], ident[:])
+            nc.scalar.copy(out=state_t[:, half * BANK : (half + 1) * BANK], in_=bank[:])
+        state_pairs = state_t[:].bitcast(BF16).rearrange("p (j k e) -> p j k e", j=UNITS, e=PAIR)
+
+        h_codes = keep.tile([P, PASSES * TOKENS], U32, align_bytes=64)
+        h_scales = keep.tile([P, PASSES * TOKENS], U8, align_bytes=64)
+
+        quantised = {}
+        per_pass = {}
+
+        def transpose_and_quantise(r):
+            quantised[r] = []
+            for n, (w, j, e) in enumerate(rounds[r]):
+                grouped = grouped_pool.tile([P, PASSES * P * PACK], BF16, align_bytes=64)
+                grouped_words = grouped[:].bitcast(F32).rearrange("p (g c u) -> p g c u", g=PASSES, u=PAIR)
+                for half in range(CHUNK_BANKS):
+                    bank = banks.tile([P, BANK], F32, tag="bank")
+                    for q in range(BANK_BLOCKS):
+                        first = e * ROW_WORDS + half * BANK + q * P
+                        nc.tensor.transpose(bank[:, q * P : (q + 1) * P], raw_words[(w, j)][:, first : first + P], ident[:])
+                    source = bank[:].rearrange("p (g u c) -> p g c u", g=PAIR, u=PAIR)
+                    target = grouped_words[:, PAIR * half : PAIR * half + PAIR, :, :]
+                    if n == 0 and half == 0:
+                        nc.vector.tensor_copy(out=target, in_=source)
+                    else:
+                        nc.scalar.copy(out=target, in_=source)
+                codes = codes_pool.tile([P, PASSES * P], U32, align_bytes=64)
+                scales = codes_pool.tile([P, PASSES * P], U8, align_bytes=64)
+                nc.vector.quantize_mx(out=codes[:].bitcast(FP8X4), scales=scales[:], in_=grouped[:])
+                quantised[r].append((codes, scales))
+
+        def contract(target, stationary, moving):
+            for g in range(PASSES):
+                cols = slice(g * P, (g + 1) * P)
+                nc.tensor.matmul_mx(
+                    out=target,
+                    lhsT=stationary[0][:, cols].bitcast(FP8X4),
+                    lhsT_scale=stationary[1][:, cols],
+                    rhs=moving[0][:, cols].bitcast(FP8X4),
+                    rhs_scale=moving[1][:, cols],
+                    start=(g == 0),
+                    stop=(g == PASSES - 1),
+                )
+
+        def state_round(r):
+            w, j, e = rounds[r][0]
+            g, value = j // PAIR, PAIR * (j % PAIR) + e
+            kvr = sums.tile([P, 3, TOKENS], F32, tag="sums")
+            for n in range(3):
+                contract(kvr[:, n, :], quantised[r][n], (xm_codes, xm_scales))
+            if value == 0:
+                gate = work.tile([P, PACK, TOKENS], F32)
+                new_state_t = work.tile([P, PACK, TOKENS], F32)
+                per_pass[g] = (gate, new_state_t)
+            gate, new_state_t = per_pass[g]
+            nc.scalar.activation(out=gate[:, value, :], in_=kvr[:, 2, :], func=ACT.Sigmoid)
+            k_sb = work.tile([P, TOKENS], F32)
+            nc.scalar.copy(out=k_sb[:], in_=kvr[:, 0, :])
+            kv = work.tile([P, TOKENS], F32)
+            nc.vector.tensor_tensor(out=kv[:], in0=kvr[:, 1, :], in1=k_sb[:], op=MULT)
+            nc.vector.scalar_tensor_tensor(
+                out=new_state_t[:, value, :],
+                in0=state_pairs[:, j, :, e],
+                scalar=decay[:, PAIR * j + e : PAIR * j + e + 1],
+                in1=kv[:],
+                op0=MULT,
+                op1=ADD,
+            )
+            if value == PACK - 1:
+                h_grouped = work.tile([P, TOKENS, PACK], BF16, align_bytes=64)
+                nc.vector.tensor_tensor(
+                    out=h_grouped[:],
+                    in0=gate[:].rearrange("p t k -> p k t"),
+                    in1=new_state_t[:].rearrange("p t k -> p k t"),
+                    op=MULT,
+                )
+                cols = slice(g * TOKENS, (g + 1) * TOKENS)
+                nc.vector.quantize_mx(
+                    out=h_codes[:, cols].bitcast(FP8X4),
+                    scales=h_scales[:, cols],
+                    in_=h_grouped[:].rearrange("p k t -> p (k t)"),
+                )
+
+        def store_new_state(g):
+            new_state_t = per_pass[g][1]
+            bank = banks.tile([P, BANK], F32, tag="bank")
+            for value in range(PACK):
+                nc.tensor.transpose(bank[:, value * P : (value + 1) * P], new_state_t[:, value, :], ident[:])
+            natural = stores.tile([P, BANK], F32)
+            nc.vector.tensor_copy(
+                out=natural[:].rearrange("k (u c e) -> k u c e", u=PAIR, e=PAIR),
+                in_=bank[:].rearrange("k (u e c) -> k u c e", u=PAIR, e=PAIR),
+            )
+            nc.sync.dma_start(out=new_state_rows[:, g * BANK : (g + 1) * BANK], in_=natural[:])
+
+        def out_round(r):
+            j = rounds[r][0][1]
+            product = sums.tile([P, PAIR, P], F32, tag="sums")
+            for e in range(PAIR):
+                contract(product[:, e, :], (h_codes, h_scales), quantised[r][e])
+            out_sb = stores.tile([P, PAIR * P], F32)
+            nc.scalar.copy(
+                out=out_sb[:].rearrange("k (c e) -> k c e", e=PAIR),
+                in_=product[:].rearrange("k e c -> k c e"),
+            )
+            nc.sync.dma_start(out=out_rows[:, j * PAIR * P : (j + 1) * PAIR * P], in_=out_sb[:])
+
+        for i in range(len(rounds) + 1):
+            if i + LOAD_AHEAD < len(rounds):
+                load_round(i + LOAD_AHEAD)
+            if i < len(rounds):
+                transpose_and_quantise(i)
+            if i >= 2 and i - 2 < first_out_round and (i - 2) % PACK == PACK - 1:
+                store_new_state((i - 2) // PACK)
+            if i >= 1:
+                if i - 1 < first_out_round:
+                    state_round(i - 1)
+                else:
+                    out_round(i - 1)

@@ -24,8 +24,13 @@ ROW_WORDS = CHANNELS // PAIR
 BANK = 512
 BANK_BLOCKS = BANK // P
 CHUNK_BANKS = ROW_WORDS // BANK
-LOAD_AHEAD = 6
 RAW_BUFS = 12
+LOAD_AHEAD = RAW_BUFS - 1
+LAG = 2
+KEY = 0
+VALUE = 1
+RECEPTANCE = 2
+OUTPUT = 3
 
 FLOPS = 4 * 2 * TOKENS * CHANNELS * CHANNELS
 
@@ -36,20 +41,19 @@ def tile_rwkvtimemix_pa_kernel(tc, x, state, Wk, Wv, Wr, Wo, time_decay, time_cu
     out_rows = out_0.rearrange("b t d -> (b t) d")
     new_state_rows = out_1.rearrange("b t d -> (b t) d")
 
-    rounds = []
+    units = []
     for j in range(UNITS):
-        for e in range(PAIR):
-            rounds.append([(0, j, e), (1, j, e), (2, j, e)])
-    first_out_round = len(rounds)
+        units.extend([(KEY, j), (VALUE, j), (RECEPTANCE, j)])
+    first_out_unit = len(units)
     for j in range(UNITS):
-        rounds.append([(3, j, 0), (3, j, 1)])
+        units.append((OUTPUT, j))
 
     with ExitStack() as ctx:
         ctx.enter_context(tc.manual_schedule())
         keep = ctx.enter_context(tc.tile_pool(name="keep", bufs=1))
         raw_pool = ctx.enter_context(tc.tile_pool(name="raw", bufs=RAW_BUFS))
         grouped_pool = ctx.enter_context(tc.tile_pool(name="grouped", bufs=4))
-        codes_pool = ctx.enter_context(tc.tile_pool(name="codes", bufs=6))
+        codes_pool = ctx.enter_context(tc.tile_pool(name="codes", bufs=PAIR * (LAG + 1)))
         work = ctx.enter_context(tc.tile_pool(name="work", bufs=2))
         stores = ctx.enter_context(tc.tile_pool(name="stores", bufs=4))
         banks = ctx.enter_context(tc.psum_pool(name="banks", bufs=6))
@@ -76,16 +80,15 @@ def tile_rwkvtimemix_pa_kernel(tc, x, state, Wk, Wv, Wr, Wo, time_decay, time_cu
 
         raw_words = {}
 
-        def load_round(r):
-            for w, j, e in rounds[r]:
-                if (w, j) not in raw_words:
-                    raw = raw_pool.tile([P, PAIR * CHANNELS], BF16)
-                    unit_rows = weights[w][j * P * PAIR : (j + 1) * P * PAIR, :]
-                    nc.sync.dma_start(out=raw[:], in_=unit_rows.rearrange("(p e) k -> p (e k)", e=PAIR))
-                    raw_words[(w, j)] = raw[:].bitcast(F32)
+        def load_unit(n):
+            w, j = units[n]
+            raw = raw_pool.tile([P, PAIR * CHANNELS], BF16)
+            unit_rows = weights[w][j * P * PAIR : (j + 1) * P * PAIR, :]
+            nc.sync.dma_start(out=raw[:], in_=unit_rows.rearrange("(p e) k -> p (e k)", e=PAIR))
+            raw_words[n] = raw[:].bitcast(F32)
 
-        for r in range(LOAD_AHEAD):
-            load_round(r)
+        for n in range(LOAD_AHEAD):
+            load_unit(n)
 
         bank = banks.tile([P, BANK], F32, tag="bank")
         nc.tensor.transpose(bank[:, 0:P], vectors[:].bitcast(F32), ident[:])
@@ -99,8 +102,8 @@ def tile_rwkvtimemix_pa_kernel(tc, x, state, Wk, Wv, Wr, Wo, time_decay, time_cu
         decay = keep.tile([P, UNITS * PAIR], F32)
         nc.scalar.activation(out=decay[:], in_=exp_decay[:], func=ACT.Exp, scale=-1.0)
 
-        def over_tokens(columns, units):
-            pairs = columns.rearrange("p (j e) -> p j e", e=PAIR)[:, units, :]
+        def over_tokens(columns, four_j):
+            pairs = columns.rearrange("p (j e) -> p j e", e=PAIR)[:, four_j, :]
             return pairs.unsqueeze(2).to_broadcast([P, BANK_BLOCKS, TOKENS, PAIR])
 
         x_words = x_sb[:].bitcast(F32)
@@ -108,7 +111,7 @@ def tile_rwkvtimemix_pa_kernel(tc, x, state, Wk, Wv, Wr, Wo, time_decay, time_cu
         before_part = keep.tile([P, UNITS, TOKENS, PAIR], F32)
         xm_grouped = keep.tile([P, PASSES, TOKENS, PACK], BF16, align_bytes=64)
         for half in range(UNITS // BANK_BLOCKS):
-            units = slice(half * BANK_BLOCKS, (half + 1) * BANK_BLOCKS)
+            four_j = slice(half * BANK_BLOCKS, (half + 1) * BANK_BLOCKS)
             now = banks.tile([P, BANK], F32, tag="bank")
             before = banks.tile([P, BANK], F32, tag="bank")
             for target, mover in ((now, ident), (before, shift)):
@@ -116,15 +119,15 @@ def tile_rwkvtimemix_pa_kernel(tc, x, state, Wk, Wv, Wr, Wo, time_decay, time_cu
                     j = half * BANK_BLOCKS + q
                     nc.tensor.transpose(target[:, q * P : (q + 1) * P], x_words[:, j * P : (j + 1) * P], mover[:])
             nc.vector.tensor_tensor(
-                out=now_part[:, units, :, :],
+                out=now_part[:, four_j, :, :],
                 in0=now[:].bitcast(BF16).rearrange("p (j k e) -> p j k e", j=BANK_BLOCKS, e=PAIR),
-                in1=over_tokens(curve, units),
+                in1=over_tokens(curve, four_j),
                 op=MULT,
             )
             nc.vector.tensor_tensor(
-                out=before_part[:, units, :, :],
+                out=before_part[:, four_j, :, :],
                 in0=before[:].bitcast(BF16).rearrange("p (j k e) -> p j k e", j=BANK_BLOCKS, e=PAIR),
-                in1=over_tokens(one_minus_curve[:], units),
+                in1=over_tokens(one_minus_curve[:], four_j),
                 op=MULT,
             )
             for g in range(half * BANK_BLOCKS // PAIR, (half + 1) * BANK_BLOCKS // PAIR):
@@ -156,28 +159,30 @@ def tile_rwkvtimemix_pa_kernel(tc, x, state, Wk, Wv, Wr, Wo, time_decay, time_cu
         h_scales = keep.tile([P, PASSES * TOKENS], U8, align_bytes=64)
 
         quantised = {}
+        sums_of = {}
+        kv_of = {}
         per_pass = {}
 
-        def transpose_and_quantise(r):
-            quantised[r] = []
-            for n, (w, j, e) in enumerate(rounds[r]):
+        def transpose_and_quantise(n):
+            quantised[n] = []
+            for e in range(PAIR):
                 grouped = grouped_pool.tile([P, PASSES * P * PACK], BF16, align_bytes=64)
                 grouped_words = grouped[:].bitcast(F32).rearrange("p (g c u) -> p g c u", g=PASSES, u=PAIR)
                 for half in range(CHUNK_BANKS):
                     bank = banks.tile([P, BANK], F32, tag="bank")
                     for q in range(BANK_BLOCKS):
                         first = e * ROW_WORDS + half * BANK + q * P
-                        nc.tensor.transpose(bank[:, q * P : (q + 1) * P], raw_words[(w, j)][:, first : first + P], ident[:])
+                        nc.tensor.transpose(bank[:, q * P : (q + 1) * P], raw_words[n][:, first : first + P], ident[:])
                     source = bank[:].rearrange("p (g u c) -> p g c u", g=PAIR, u=PAIR)
                     target = grouped_words[:, PAIR * half : PAIR * half + PAIR, :, :]
-                    if n == 0 and half == 0:
+                    if e == 0 and half == 0:
                         nc.vector.tensor_copy(out=target, in_=source)
                     else:
                         nc.scalar.copy(out=target, in_=source)
                 codes = codes_pool.tile([P, PASSES * P], U32, align_bytes=64)
                 scales = codes_pool.tile([P, PASSES * P], U8, align_bytes=64)
                 nc.vector.quantize_mx(out=codes[:].bitcast(FP8X4), scales=scales[:], in_=grouped[:])
-                quantised[r].append((codes, scales))
+                quantised[n].append((codes, scales))
 
         def contract(target, stationary, moving):
             for g in range(PASSES):
@@ -192,31 +197,41 @@ def tile_rwkvtimemix_pa_kernel(tc, x, state, Wk, Wv, Wr, Wo, time_decay, time_cu
                     stop=(g == PASSES - 1),
                 )
 
-        def state_round(r):
-            w, j, e = rounds[r][0]
-            g, value = j // PAIR, PAIR * (j % PAIR) + e
-            kvr = sums.tile([P, 3, TOKENS], F32, tag="sums")
-            for n in range(3):
-                contract(kvr[:, n, :], quantised[r][n], (xm_codes, xm_scales))
-            if value == 0:
+
+        def key_unit(n, j):
+            sums_of[j] = sums.tile([P, 2 * PAIR, TOKENS], F32, tag="sum", name="k_and_v")
+            for e in range(PAIR):
+                contract(sums_of[j][:, e, :], quantised[n][e], (xm_codes, xm_scales))
+
+        def value_unit(n, j):
+            for e in range(PAIR):
+                contract(sums_of[j][:, PAIR + e, :], quantised[n][e], (xm_codes, xm_scales))
+            k_sb = work.tile([P, PAIR, TOKENS], F32)
+            nc.scalar.copy(out=k_sb[:], in_=sums_of[j][:, 0:PAIR, :])
+            kv_of[j] = work.tile([P, PAIR, TOKENS], F32, name="kv")
+            nc.vector.tensor_tensor(out=kv_of[j][:], in0=sums_of[j][:, PAIR : 2 * PAIR, :], in1=k_sb[:], op=MULT)
+
+        def receptance_unit(n, j):
+            g, u = j // PAIR, j % PAIR
+            r_sum = sums.tile([P, PAIR, TOKENS], F32, tag="sum")
+            for e in range(PAIR):
+                contract(r_sum[:, e, :], quantised[n][e], (xm_codes, xm_scales))
+            if u == 0:
                 gate = work.tile([P, PACK, TOKENS], F32)
                 new_state_t = work.tile([P, PACK, TOKENS], F32)
                 per_pass[g] = (gate, new_state_t)
             gate, new_state_t = per_pass[g]
-            nc.scalar.activation(out=gate[:, value, :], in_=kvr[:, 2, :], func=ACT.Sigmoid)
-            k_sb = work.tile([P, TOKENS], F32)
-            nc.scalar.copy(out=k_sb[:], in_=kvr[:, 0, :])
-            kv = work.tile([P, TOKENS], F32)
-            nc.vector.tensor_tensor(out=kv[:], in0=kvr[:, 1, :], in1=k_sb[:], op=MULT)
-            nc.vector.scalar_tensor_tensor(
-                out=new_state_t[:, value, :],
-                in0=state_pairs[:, j, :, e],
-                scalar=decay[:, PAIR * j + e : PAIR * j + e + 1],
-                in1=kv[:],
-                op0=MULT,
-                op1=ADD,
-            )
-            if value == PACK - 1:
+            nc.scalar.activation(out=gate[:, PAIR * u : PAIR * u + PAIR, :], in_=r_sum[:], func=ACT.Sigmoid)
+            for e in range(PAIR):
+                nc.vector.scalar_tensor_tensor(
+                    out=new_state_t[:, PAIR * u + e, :],
+                    in0=state_pairs[:, j, :, e],
+                    scalar=decay[:, PAIR * j + e : PAIR * j + e + 1],
+                    in1=kv_of[j][:, e, :],
+                    op0=MULT,
+                    op1=ADD,
+                )
+            if u == PAIR - 1:
                 h_grouped = work.tile([P, TOKENS, PACK], BF16, align_bytes=64)
                 nc.vector.tensor_tensor(
                     out=h_grouped[:],
@@ -237,17 +252,16 @@ def tile_rwkvtimemix_pa_kernel(tc, x, state, Wk, Wv, Wr, Wo, time_decay, time_cu
             for value in range(PACK):
                 nc.tensor.transpose(bank[:, value * P : (value + 1) * P], new_state_t[:, value, :], ident[:])
             natural = stores.tile([P, BANK], F32)
-            nc.vector.tensor_copy(
+            nc.scalar.copy(
                 out=natural[:].rearrange("k (u c e) -> k u c e", u=PAIR, e=PAIR),
                 in_=bank[:].rearrange("k (u e c) -> k u c e", u=PAIR, e=PAIR),
             )
             nc.sync.dma_start(out=new_state_rows[:, g * BANK : (g + 1) * BANK], in_=natural[:])
 
-        def out_round(r):
-            j = rounds[r][0][1]
-            product = sums.tile([P, PAIR, P], F32, tag="sums")
+        def out_unit(n, j):
+            product = sums.tile([P, PAIR, P], F32, tag="sum")
             for e in range(PAIR):
-                contract(product[:, e, :], (h_codes, h_scales), quantised[r][e])
+                contract(product[:, e, :], (h_codes, h_scales), quantised[n][e])
             out_sb = stores.tile([P, PAIR * P], F32)
             nc.scalar.copy(
                 out=out_sb[:].rearrange("k (c e) -> k c e", e=PAIR),
@@ -255,15 +269,22 @@ def tile_rwkvtimemix_pa_kernel(tc, x, state, Wk, Wv, Wr, Wo, time_decay, time_cu
             )
             nc.sync.dma_start(out=out_rows[:, j * PAIR * P : (j + 1) * PAIR * P], in_=out_sb[:])
 
-        for i in range(len(rounds) + 1):
-            if i + LOAD_AHEAD < len(rounds):
-                load_round(i + LOAD_AHEAD)
-            if i < len(rounds):
+        units_of_a_pass = 3 * PAIR
+        for i in range(len(units) + LAG):
+            if i + LOAD_AHEAD < len(units):
+                load_unit(i + LOAD_AHEAD)
+            if i < len(units):
                 transpose_and_quantise(i)
-            if i >= 2 and i - 2 < first_out_round and (i - 2) % PACK == PACK - 1:
-                store_new_state((i - 2) // PACK)
-            if i >= 1:
-                if i - 1 < first_out_round:
-                    state_round(i - 1)
+            n = i - LAG - 2
+            if 0 <= n < first_out_unit and n % units_of_a_pass == units_of_a_pass - 1:
+                store_new_state(n // units_of_a_pass)
+            if i >= LAG:
+                w, j = units[i - LAG]
+                if w == KEY:
+                    key_unit(i - LAG, j)
+                elif w == VALUE:
+                    value_unit(i - LAG, j)
+                elif w == RECEPTANCE:
+                    receptance_unit(i - LAG, j)
                 else:
-                    out_round(i - 1)
+                    out_unit(i - LAG, j)

@@ -26,7 +26,6 @@ BANK_BLOCKS = BANK // P
 CHUNK_BANKS = ROW_WORDS // BANK
 RAW_BUFS = 12
 LOAD_AHEAD = RAW_BUFS - 1
-LAG = 2
 KEY = 0
 VALUE = 1
 RECEPTANCE = 2
@@ -53,7 +52,7 @@ def tile_rwkvtimemix_pa_kernel(tc, x, state, Wk, Wv, Wr, Wo, time_decay, time_cu
         keep = ctx.enter_context(tc.tile_pool(name="keep", bufs=1))
         raw_pool = ctx.enter_context(tc.tile_pool(name="raw", bufs=RAW_BUFS))
         grouped_pool = ctx.enter_context(tc.tile_pool(name="grouped", bufs=4))
-        codes_pool = ctx.enter_context(tc.tile_pool(name="codes", bufs=PAIR * (LAG + 1)))
+        codes_pool = ctx.enter_context(tc.tile_pool(name="codes", bufs=3 * PAIR))
         work = ctx.enter_context(tc.tile_pool(name="work", bufs=2))
         stores = ctx.enter_context(tc.tile_pool(name="stores", bufs=4))
         banks = ctx.enter_context(tc.psum_pool(name="banks", bufs=6))
@@ -158,13 +157,15 @@ def tile_rwkvtimemix_pa_kernel(tc, x, state, Wk, Wv, Wr, Wo, time_decay, time_cu
         h_codes = keep.tile([P, PASSES * TOKENS], U32, align_bytes=64)
         h_scales = keep.tile([P, PASSES * TOKENS], U8, align_bytes=64)
 
+        grouped_of = {}
         quantised = {}
         sums_of = {}
+        k_of = {}
         kv_of = {}
         per_pass = {}
 
-        def transpose_and_quantise(n):
-            quantised[n] = []
+        def transpose(n):
+            grouped_of[n] = []
             for e in range(PAIR):
                 grouped = grouped_pool.tile([P, PASSES * P * PACK], BF16, align_bytes=64)
                 grouped_words = grouped[:].bitcast(F32).rearrange("p (g c u) -> p g c u", g=PASSES, u=PAIR)
@@ -179,6 +180,11 @@ def tile_rwkvtimemix_pa_kernel(tc, x, state, Wk, Wv, Wr, Wo, time_decay, time_cu
                         nc.vector.tensor_copy(out=target, in_=source)
                     else:
                         nc.scalar.copy(out=target, in_=source)
+                grouped_of[n].append(grouped)
+
+        def quantise(n):
+            quantised[n] = []
+            for grouped in grouped_of[n]:
                 codes = codes_pool.tile([P, PASSES * P], U32, align_bytes=64)
                 scales = codes_pool.tile([P, PASSES * P], U8, align_bytes=64)
                 nc.vector.quantize_mx(out=codes[:].bitcast(FP8X4), scales=scales[:], in_=grouped[:])
@@ -197,54 +203,72 @@ def tile_rwkvtimemix_pa_kernel(tc, x, state, Wk, Wv, Wr, Wo, time_decay, time_cu
                     stop=(g == PASSES - 1),
                 )
 
+        def multiply(n):
+            w, j = units[n]
+            if w == VALUE:
+                sums_of[n] = sums_of[n - 1]
+            else:
+                sums_of[n] = sums.tile([P, 2 * PAIR, TOKENS], F32, tag="sum", name="products")
+            for e in range(PAIR):
+                if w == OUTPUT:
+                    contract(sums_of[n][:, e, :], (h_codes, h_scales), quantised[n][e])
+                elif w == VALUE:
+                    contract(sums_of[n][:, PAIR + e, :], quantised[n][e], (xm_codes, xm_scales))
+                else:
+                    contract(sums_of[n][:, e, :], quantised[n][e], (xm_codes, xm_scales))
 
-        def key_unit(n, j):
-            sums_of[j] = sums.tile([P, 2 * PAIR, TOKENS], F32, tag="sum", name="k_and_v")
-            for e in range(PAIR):
-                contract(sums_of[j][:, e, :], quantised[n][e], (xm_codes, xm_scales))
+        def finish_on_scalar(n):
+            w, j = units[n]
+            if w == VALUE:
+                k_of[j] = work.tile([P, PAIR, TOKENS], F32, name="k_sb")
+                nc.scalar.copy(out=k_of[j][:], in_=sums_of[n][:, 0:PAIR, :])
+            elif w == RECEPTANCE:
+                g, u = j // PAIR, j % PAIR
+                if u == 0:
+                    gate = work.tile([P, PACK, TOKENS], F32)
+                    new_state_t = work.tile([P, PACK, TOKENS], F32)
+                    per_pass[g] = (gate, new_state_t)
+                gate = per_pass[g][0]
+                nc.scalar.activation(out=gate[:, PAIR * u : PAIR * u + PAIR, :], in_=sums_of[n][:, 0:PAIR, :], func=ACT.Sigmoid)
+            elif w == OUTPUT:
+                out_sb = stores.tile([P, PAIR * P], F32)
+                nc.scalar.copy(
+                    out=out_sb[:].rearrange("k (c e) -> k c e", e=PAIR),
+                    in_=sums_of[n][:, 0:PAIR, :].rearrange("k e c -> k c e"),
+                )
+                nc.sync.dma_start(out=out_rows[:, j * PAIR * P : (j + 1) * PAIR * P], in_=out_sb[:])
 
-        def value_unit(n, j):
-            for e in range(PAIR):
-                contract(sums_of[j][:, PAIR + e, :], quantised[n][e], (xm_codes, xm_scales))
-            k_sb = work.tile([P, PAIR, TOKENS], F32)
-            nc.scalar.copy(out=k_sb[:], in_=sums_of[j][:, 0:PAIR, :])
-            kv_of[j] = work.tile([P, PAIR, TOKENS], F32, name="kv")
-            nc.vector.tensor_tensor(out=kv_of[j][:], in0=sums_of[j][:, PAIR : 2 * PAIR, :], in1=k_sb[:], op=MULT)
-
-        def receptance_unit(n, j):
-            g, u = j // PAIR, j % PAIR
-            r_sum = sums.tile([P, PAIR, TOKENS], F32, tag="sum")
-            for e in range(PAIR):
-                contract(r_sum[:, e, :], quantised[n][e], (xm_codes, xm_scales))
-            if u == 0:
-                gate = work.tile([P, PACK, TOKENS], F32)
-                new_state_t = work.tile([P, PACK, TOKENS], F32)
-                per_pass[g] = (gate, new_state_t)
-            gate, new_state_t = per_pass[g]
-            nc.scalar.activation(out=gate[:, PAIR * u : PAIR * u + PAIR, :], in_=r_sum[:], func=ACT.Sigmoid)
-            for e in range(PAIR):
-                nc.vector.scalar_tensor_tensor(
-                    out=new_state_t[:, PAIR * u + e, :],
-                    in0=state_pairs[:, j, :, e],
-                    scalar=decay[:, PAIR * j + e : PAIR * j + e + 1],
-                    in1=kv_of[j][:, e, :],
-                    op0=MULT,
-                    op1=ADD,
-                )
-            if u == PAIR - 1:
-                h_grouped = work.tile([P, TOKENS, PACK], BF16, align_bytes=64)
-                nc.vector.tensor_tensor(
-                    out=h_grouped[:],
-                    in0=gate[:].rearrange("p t k -> p k t"),
-                    in1=new_state_t[:].rearrange("p t k -> p k t"),
-                    op=MULT,
-                )
-                cols = slice(g * TOKENS, (g + 1) * TOKENS)
-                nc.vector.quantize_mx(
-                    out=h_codes[:, cols].bitcast(FP8X4),
-                    scales=h_scales[:, cols],
-                    in_=h_grouped[:].rearrange("p k t -> p (k t)"),
-                )
+        def finish_on_vector(n):
+            w, j = units[n]
+            if w == VALUE:
+                kv_of[j] = work.tile([P, PAIR, TOKENS], F32, name="kv")
+                nc.vector.tensor_tensor(out=kv_of[j][:], in0=sums_of[n][:, PAIR : 2 * PAIR, :], in1=k_of[j][:], op=MULT)
+            elif w == RECEPTANCE:
+                g, u = j // PAIR, j % PAIR
+                gate, new_state_t = per_pass[g]
+                for e in range(PAIR):
+                    nc.vector.scalar_tensor_tensor(
+                        out=new_state_t[:, PAIR * u + e, :],
+                        in0=state_pairs[:, j, :, e],
+                        scalar=decay[:, PAIR * j + e : PAIR * j + e + 1],
+                        in1=kv_of[j][:, e, :],
+                        op0=MULT,
+                        op1=ADD,
+                    )
+                if u == PAIR - 1:
+                    h_grouped = work.tile([P, TOKENS, PACK], BF16, align_bytes=64)
+                    nc.vector.tensor_tensor(
+                        out=h_grouped[:],
+                        in0=gate[:].rearrange("p t k -> p k t"),
+                        in1=new_state_t[:].rearrange("p t k -> p k t"),
+                        op=MULT,
+                    )
+                    cols = slice(g * TOKENS, (g + 1) * TOKENS)
+                    nc.vector.quantize_mx(
+                        out=h_codes[:, cols].bitcast(FP8X4),
+                        scales=h_scales[:, cols],
+                        in_=h_grouped[:].rearrange("p k t -> p (k t)"),
+                    )
 
         def store_new_state(g):
             new_state_t = per_pass[g][1]
@@ -258,33 +282,22 @@ def tile_rwkvtimemix_pa_kernel(tc, x, state, Wk, Wv, Wr, Wo, time_decay, time_cu
             )
             nc.sync.dma_start(out=new_state_rows[:, g * BANK : (g + 1) * BANK], in_=natural[:])
 
-        def out_unit(n, j):
-            product = sums.tile([P, PAIR, P], F32, tag="sum")
-            for e in range(PAIR):
-                contract(product[:, e, :], (h_codes, h_scales), quantised[n][e])
-            out_sb = stores.tile([P, PAIR * P], F32)
-            nc.scalar.copy(
-                out=out_sb[:].rearrange("k (c e) -> k c e", e=PAIR),
-                in_=product[:].rearrange("k e c -> k c e"),
-            )
-            nc.sync.dma_start(out=out_rows[:, j * PAIR * P : (j + 1) * PAIR * P], in_=out_sb[:])
-
+        multiply_order = list(range(first_out_unit)) + [None] + list(range(first_out_unit, len(units)))
         units_of_a_pass = 3 * PAIR
-        for i in range(len(units) + LAG):
+        for i in range(len(multiply_order) + 3):
             if i + LOAD_AHEAD < len(units):
                 load_unit(i + LOAD_AHEAD)
+            finishing = multiply_order[i - 3] if 3 <= i else None
+            if finishing is not None:
+                finish_on_scalar(finishing)
             if i < len(units):
-                transpose_and_quantise(i)
-            n = i - LAG - 2
+                transpose(i)
+            if 1 <= i <= len(units):
+                quantise(i - 1)
+            if finishing is not None:
+                finish_on_vector(finishing)
+            n = i - 5
             if 0 <= n < first_out_unit and n % units_of_a_pass == units_of_a_pass - 1:
                 store_new_state(n // units_of_a_pass)
-            if i >= LAG:
-                w, j = units[i - LAG]
-                if w == KEY:
-                    key_unit(i - LAG, j)
-                elif w == VALUE:
-                    value_unit(i - LAG, j)
-                elif w == RECEPTANCE:
-                    receptance_unit(i - LAG, j)
-                else:
-                    out_unit(i - LAG, j)
+            if 2 <= i < len(multiply_order) + 2 and multiply_order[i - 2] is not None:
+                multiply(multiply_order[i - 2])

@@ -26,6 +26,11 @@ BANK_BLOCKS = BANK // P
 CHUNK_BANKS = ROW_WORDS // BANK
 RAW_BUFS = 12
 LOAD_AHEAD = RAW_BUFS - 1
+QUANTISE_AFTER = 1
+MULTIPLY_AFTER = 3
+FINISH_AFTER = 4
+RETURN_AFTER = 6
+VECTOR_JOINS_AT = 3
 KEY = 0
 VALUE = 1
 RECEPTANCE = 2
@@ -52,12 +57,14 @@ def tile_rwkvtimemix_pa_kernel(tc, x, state, Wk, Wv, Wr, Wo, time_decay, time_cu
         keep = ctx.enter_context(tc.tile_pool(name="keep", bufs=1))
         raw_pool = ctx.enter_context(tc.tile_pool(name="raw", bufs=RAW_BUFS))
         grouped_pool = ctx.enter_context(tc.tile_pool(name="grouped", bufs=4))
-        codes_pool = ctx.enter_context(tc.tile_pool(name="codes", bufs=3 * PAIR))
+        codes_pool = ctx.enter_context(tc.tile_pool(name="codes", bufs=PAIR * (MULTIPLY_AFTER - QUANTISE_AFTER + 2)))
         work = ctx.enter_context(tc.tile_pool(name="work", bufs=2))
         stores = ctx.enter_context(tc.tile_pool(name="stores", bufs=4))
         banks = ctx.enter_context(tc.psum_pool(name="banks", bufs=6))
         sums = ctx.enter_context(tc.psum_pool(name="sums", bufs=2))
 
+        x_sb = keep.tile([P, CHANNELS], BF16)
+        nc.sync.dma_start(out=x_sb[:], in_=x.rearrange("b t d -> (b t) d"))
         vectors = keep.tile([P, P * PAIR], BF16)
         nc.vector.memset(vectors[:], 0.0)
         nc.sync.dma_start(out=vectors[0:UNITS, :], in_=time_curve.rearrange("(j c) -> j c", j=UNITS))
@@ -72,8 +79,6 @@ def tile_rwkvtimemix_pa_kernel(tc, x, state, Wk, Wv, Wr, Wo, time_decay, time_cu
             in_=ident[:].rearrange("p (b t) -> p b t", t=SEQ_LEN)[:, :, 0 : SEQ_LEN - 1],
         )
 
-        x_sb = keep.tile([P, CHANNELS], BF16)
-        nc.sync.dma_start(out=x_sb[:], in_=x.rearrange("b t d -> (b t) d"))
         state_sb = keep.tile([P, CHANNELS], BF16)
         nc.sync.dma_start(out=state_sb[:], in_=state.rearrange("b t d -> (b t) d"))
 
@@ -83,7 +88,14 @@ def tile_rwkvtimemix_pa_kernel(tc, x, state, Wk, Wv, Wr, Wo, time_decay, time_cu
             w, j = units[n]
             raw = raw_pool.tile([P, PAIR * CHANNELS], BF16)
             unit_rows = weights[w][j * P * PAIR : (j + 1) * P * PAIR, :]
-            nc.sync.dma_start(out=raw[:], in_=unit_rows.rearrange("(p e) k -> p (e k)", e=PAIR))
+            if n < len(units) - 1:
+                nc.sync.dma_start(out=raw[:], in_=unit_rows.rearrange("(p e) k -> p (e k)", e=PAIR))
+            else:
+                for e in range(PAIR):
+                    nc.sync.dma_start(
+                        out=raw[:, e * CHANNELS : (e + 1) * CHANNELS],
+                        in_=unit_rows.rearrange("(p e) k -> e p k", e=PAIR)[e],
+                    )
             raw_words[n] = raw[:].bitcast(F32)
 
         for n in range(LOAD_AHEAD):
@@ -176,7 +188,7 @@ def tile_rwkvtimemix_pa_kernel(tc, x, state, Wk, Wv, Wr, Wo, time_decay, time_cu
                         nc.tensor.transpose(bank[:, q * P : (q + 1) * P], raw_words[n][:, first : first + P], ident[:])
                     source = bank[:].rearrange("p (g u c) -> p g c u", g=PAIR, u=PAIR)
                     target = grouped_words[:, PAIR * half : PAIR * half + PAIR, :, :]
-                    if e == 0 and half == 0:
+                    if e == 0 and half == 0 and n >= VECTOR_JOINS_AT:
                         nc.vector.tensor_copy(out=target, in_=source)
                     else:
                         nc.scalar.copy(out=target, in_=source)
@@ -270,7 +282,7 @@ def tile_rwkvtimemix_pa_kernel(tc, x, state, Wk, Wv, Wr, Wo, time_decay, time_cu
                         in_=h_grouped[:].rearrange("p k t -> p (k t)"),
                     )
 
-        def store_new_state(g):
+        def return_new_state(g):
             new_state_t = per_pass[g][1]
             bank = banks.tile([P, BANK], F32, tag="bank")
             for value in range(PACK):
@@ -280,24 +292,29 @@ def tile_rwkvtimemix_pa_kernel(tc, x, state, Wk, Wv, Wr, Wo, time_decay, time_cu
                 out=natural[:].rearrange("k (u c e) -> k u c e", u=PAIR, e=PAIR),
                 in_=bank[:].rearrange("k (u e c) -> k u c e", u=PAIR, e=PAIR),
             )
-            nc.sync.dma_start(out=new_state_rows[:, g * BANK : (g + 1) * BANK], in_=natural[:])
+            return natural
 
         multiply_order = list(range(first_out_unit)) + [None] + list(range(first_out_unit, len(units)))
         units_of_a_pass = 3 * PAIR
-        for i in range(len(multiply_order) + 3):
+        returned = []
+        for i in range(len(multiply_order) + FINISH_AFTER):
             if i + LOAD_AHEAD < len(units):
                 load_unit(i + LOAD_AHEAD)
-            finishing = multiply_order[i - 3] if 3 <= i else None
+            finishing = multiply_order[i - FINISH_AFTER] if i >= FINISH_AFTER else None
             if finishing is not None:
                 finish_on_scalar(finishing)
             if i < len(units):
                 transpose(i)
-            if 1 <= i <= len(units):
-                quantise(i - 1)
+            if 0 <= i - QUANTISE_AFTER < len(units):
+                quantise(i - QUANTISE_AFTER)
             if finishing is not None:
                 finish_on_vector(finishing)
-            n = i - 5
+            n = i - RETURN_AFTER
             if 0 <= n < first_out_unit and n % units_of_a_pass == units_of_a_pass - 1:
-                store_new_state(n // units_of_a_pass)
-            if 2 <= i < len(multiply_order) + 2 and multiply_order[i - 2] is not None:
-                multiply(multiply_order[i - 2])
+                returned.append((n // units_of_a_pass, return_new_state(n // units_of_a_pass)))
+            if i + LOAD_AHEAD >= len(units) - 1:
+                for g, natural in returned:
+                    nc.sync.dma_start(out=new_state_rows[:, g * BANK : (g + 1) * BANK], in_=natural[:])
+                returned = []
+            if 0 <= i - MULTIPLY_AFTER < len(multiply_order) and multiply_order[i - MULTIPLY_AFTER] is not None:
+                multiply(multiply_order[i - MULTIPLY_AFTER])

@@ -25,11 +25,8 @@ BANK = 512
 BANK_BLOCKS = BANK // P
 CHUNK_BANKS = ROW_WORDS // BANK
 RAW_BUFS = 12
-LOAD_AHEAD = RAW_BUFS - 1
-QUANTISE_AFTER = 1
-MULTIPLY_AFTER = 3
-FINISH_AFTER = 4
-RETURN_AFTER = 6
+STEP_UNITS = 2
+LOAD_AHEAD = RAW_BUFS - STEP_UNITS
 VECTOR_JOINS_AT = 3
 KEY = 0
 VALUE = 1
@@ -45,19 +42,19 @@ def tile_rwkvtimemix_pa_kernel(tc, x, state, Wk, Wv, Wr, Wo, time_decay, time_cu
     out_rows = out_0.rearrange("b t d -> (b t) d")
     new_state_rows = out_1.rearrange("b t d -> (b t) d")
 
-    units = []
-    for j in range(UNITS):
-        units.extend([(KEY, j), (VALUE, j), (RECEPTANCE, j)])
-    first_out_unit = len(units)
-    for j in range(UNITS):
-        units.append((OUTPUT, j))
+    steps = []
+    for g in range(PASSES):
+        steps.extend([(KEY, g), (VALUE, g), (RECEPTANCE, g)])
+    for g in range(PASSES):
+        steps.append((OUTPUT, g))
+    units = [(w, STEP_UNITS * g + u) for w, g in steps for u in range(STEP_UNITS)]
 
     with ExitStack() as ctx:
         ctx.enter_context(tc.manual_schedule())
         keep = ctx.enter_context(tc.tile_pool(name="keep", bufs=1))
         raw_pool = ctx.enter_context(tc.tile_pool(name="raw", bufs=RAW_BUFS))
         grouped_pool = ctx.enter_context(tc.tile_pool(name="grouped", bufs=4))
-        codes_pool = ctx.enter_context(tc.tile_pool(name="codes", bufs=PAIR * (MULTIPLY_AFTER - QUANTISE_AFTER + 2)))
+        codes_pool = ctx.enter_context(tc.tile_pool(name="codes", bufs=3 * STEP_UNITS))
         work = ctx.enter_context(tc.tile_pool(name="work", bufs=2))
         stores = ctx.enter_context(tc.tile_pool(name="stores", bufs=4))
         banks = ctx.enter_context(tc.psum_pool(name="banks", bufs=6))
@@ -91,10 +88,12 @@ def tile_rwkvtimemix_pa_kernel(tc, x, state, Wk, Wv, Wr, Wo, time_decay, time_cu
             if n < len(units) - 1:
                 nc.sync.dma_start(out=raw[:], in_=unit_rows.rearrange("(p e) k -> p (e k)", e=PAIR))
             else:
-                for e in range(PAIR):
+                half_row = CHANNELS // CHUNK_BANKS
+                for half in range(CHUNK_BANKS):
+                    cols = slice(half * half_row, (half + 1) * half_row)
                     nc.sync.dma_start(
-                        out=raw[:, e * CHANNELS : (e + 1) * CHANNELS],
-                        in_=unit_rows.rearrange("(p e) k -> e p k", e=PAIR)[e],
+                        out=raw[:].rearrange("p (e k) -> p e k", e=PAIR)[:, :, cols],
+                        in_=unit_rows.rearrange("(p e) k -> p e k", e=PAIR)[:, :, cols],
                     )
             raw_words[n] = raw[:].bitcast(F32)
 
@@ -173,120 +172,134 @@ def tile_rwkvtimemix_pa_kernel(tc, x, state, Wk, Wv, Wr, Wo, time_decay, time_cu
         quantised = {}
         sums_of = {}
         k_of = {}
-        kv_of = {}
-        per_pass = {}
+        new_state_of = {}
+        gate_of = {}
+        h_of = {}
 
         def transpose(n):
-            grouped_of[n] = []
-            for e in range(PAIR):
-                grouped = grouped_pool.tile([P, PASSES * P * PACK], BF16, align_bytes=64)
-                grouped_words = grouped[:].bitcast(F32).rearrange("p (g c u) -> p g c u", g=PASSES, u=PAIR)
-                for half in range(CHUNK_BANKS):
+            grouped = grouped_pool.tile([P, PASSES * PAIR * P * PACK], BF16, align_bytes=64)
+            grouped_words = grouped[:].bitcast(F32).rearrange("p (g e c u) -> p g e c u", g=PASSES, e=PAIR, u=PAIR)
+            for half in range(CHUNK_BANKS):
+                for e in range(PAIR):
                     bank = banks.tile([P, BANK], F32, tag="bank")
                     for q in range(BANK_BLOCKS):
                         first = e * ROW_WORDS + half * BANK + q * P
                         nc.tensor.transpose(bank[:, q * P : (q + 1) * P], raw_words[n][:, first : first + P], ident[:])
                     source = bank[:].rearrange("p (g u c) -> p g c u", g=PAIR, u=PAIR)
-                    target = grouped_words[:, PAIR * half : PAIR * half + PAIR, :, :]
+                    target = grouped_words[:, PAIR * half : PAIR * half + PAIR, e, :, :]
                     if e == 0 and half == 0 and n >= VECTOR_JOINS_AT:
                         nc.vector.tensor_copy(out=target, in_=source)
                     else:
                         nc.scalar.copy(out=target, in_=source)
-                grouped_of[n].append(grouped)
+            grouped_of[n] = grouped
 
         def quantise(n):
-            quantised[n] = []
-            for grouped in grouped_of[n]:
-                codes = codes_pool.tile([P, PASSES * P], U32, align_bytes=64)
-                scales = codes_pool.tile([P, PASSES * P], U8, align_bytes=64)
-                nc.vector.quantize_mx(out=codes[:].bitcast(FP8X4), scales=scales[:], in_=grouped[:])
-                quantised[n].append((codes, scales))
+            codes = codes_pool.tile([P, PASSES * PAIR * P], U32, align_bytes=64)
+            scales = codes_pool.tile([P, PASSES * PAIR * P], U8, align_bytes=64)
+            for half in range(CHUNK_BANKS):
+                cols = slice(half * PASSES * P, (half + 1) * PASSES * P)
+                nc.vector.quantize_mx(
+                    out=codes[:, cols].bitcast(FP8X4),
+                    scales=scales[:, cols],
+                    in_=grouped_of[n][:, half * PASSES * P * PACK : (half + 1) * PASSES * P * PACK],
+                )
+            quantised[n] = (codes, scales)
 
         def contract(target, stationary, moving):
             for g in range(PASSES):
-                cols = slice(g * P, (g + 1) * P)
                 nc.tensor.matmul_mx(
                     out=target,
-                    lhsT=stationary[0][:, cols].bitcast(FP8X4),
-                    lhsT_scale=stationary[1][:, cols],
-                    rhs=moving[0][:, cols].bitcast(FP8X4),
-                    rhs_scale=moving[1][:, cols],
+                    lhsT=stationary[0][:, stationary[2](g)].bitcast(FP8X4),
+                    lhsT_scale=stationary[1][:, stationary[2](g)],
+                    rhs=moving[0][:, moving[2](g)].bitcast(FP8X4),
+                    rhs_scale=moving[1][:, moving[2](g)],
                     start=(g == 0),
                     stop=(g == PASSES - 1),
                 )
 
-        def multiply(n):
-            w, j = units[n]
-            if w == VALUE:
-                sums_of[n] = sums_of[n - 1]
-            else:
-                sums_of[n] = sums.tile([P, 2 * PAIR, TOKENS], F32, tag="sum", name="products")
-            for e in range(PAIR):
+        def token_columns(g):
+            return slice(g * TOKENS, (g + 1) * TOKENS)
+
+        def unit_columns(g):
+            return slice(g * PAIR * P, (g + 1) * PAIR * P)
+
+        def chunk_columns(e):
+            return lambda g: slice((g * PAIR + e) * P, (g * PAIR + e + 1) * P)
+
+        def multiply(i):
+            w, g = steps[i]
+            sums_of[i] = sums.tile([P, PACK, TOKENS], F32, tag="sum", name="products")
+            for u in range(STEP_UNITS):
+                codes, scales = quantised[STEP_UNITS * i + u]
                 if w == OUTPUT:
-                    contract(sums_of[n][:, e, :], (h_codes, h_scales), quantised[n][e])
-                elif w == VALUE:
-                    contract(sums_of[n][:, PAIR + e, :], quantised[n][e], (xm_codes, xm_scales))
+                    contract(
+                        sums_of[i][:, PAIR * u : PAIR * u + PAIR, :].rearrange("k e c -> k (e c)"),
+                        (h_codes, h_scales, token_columns),
+                        (codes, scales, unit_columns),
+                    )
                 else:
-                    contract(sums_of[n][:, e, :], quantised[n][e], (xm_codes, xm_scales))
+                    for e in range(PAIR):
+                        contract(
+                            sums_of[i][:, PAIR * u + e, :],
+                            (codes, scales, chunk_columns(e)),
+                            (xm_codes, xm_scales, token_columns),
+                        )
 
-        def finish_on_scalar(n):
-            w, j = units[n]
-            if w == VALUE:
-                k_of[j] = work.tile([P, PAIR, TOKENS], F32, name="k_sb")
-                nc.scalar.copy(out=k_of[j][:], in_=sums_of[n][:, 0:PAIR, :])
+        def finish_on_scalar(i):
+            w, g = steps[i]
+            if w == KEY:
+                k_of[g] = work.tile([P, PACK, TOKENS], F32, name="k_sb")
+                nc.scalar.copy(out=k_of[g][:], in_=sums_of[i][:])
             elif w == RECEPTANCE:
-                g, u = j // PAIR, j % PAIR
-                if u == 0:
-                    gate = work.tile([P, PACK, TOKENS], F32)
-                    new_state_t = work.tile([P, PACK, TOKENS], F32)
-                    per_pass[g] = (gate, new_state_t)
-                gate = per_pass[g][0]
-                nc.scalar.activation(out=gate[:, PAIR * u : PAIR * u + PAIR, :], in_=sums_of[n][:, 0:PAIR, :], func=ACT.Sigmoid)
+                gate_of[g] = work.tile([P, PACK, TOKENS], F32, name="gate")
+                nc.scalar.activation(out=gate_of[g][:], in_=sums_of[i][:], func=ACT.Sigmoid)
             elif w == OUTPUT:
-                out_sb = stores.tile([P, PAIR * P], F32)
+                out_sb = stores.tile([P, BANK], F32)
                 nc.scalar.copy(
-                    out=out_sb[:].rearrange("k (c e) -> k c e", e=PAIR),
-                    in_=sums_of[n][:, 0:PAIR, :].rearrange("k e c -> k c e"),
+                    out=out_sb[:].rearrange("k (u c e) -> k u c e", u=PAIR, e=PAIR),
+                    in_=sums_of[i][:].rearrange("k (u e) c -> k u c e", u=PAIR),
                 )
-                nc.sync.dma_start(out=out_rows[:, j * PAIR * P : (j + 1) * PAIR * P], in_=out_sb[:])
+                nc.sync.dma_start(out=out_rows[:, g * BANK : (g + 1) * BANK], in_=out_sb[:])
 
-        def finish_on_vector(n):
-            w, j = units[n]
+        def begin_on_vector(i):
+            w, g = steps[i]
             if w == VALUE:
-                kv_of[j] = work.tile([P, PAIR, TOKENS], F32, name="kv")
-                nc.vector.tensor_tensor(out=kv_of[j][:], in0=sums_of[n][:, PAIR : 2 * PAIR, :], in1=k_of[j][:], op=MULT)
+                new_state_of[g] = work.tile([P, PACK, TOKENS], F32, name="new_state_t")
+                nc.vector.tensor_tensor(out=new_state_of[g][:], in0=sums_of[i][:], in1=k_of[g][:], op=MULT)
             elif w == RECEPTANCE:
-                g, u = j // PAIR, j % PAIR
-                gate, new_state_t = per_pass[g]
-                for e in range(PAIR):
-                    nc.vector.scalar_tensor_tensor(
-                        out=new_state_t[:, PAIR * u + e, :],
-                        in0=state_pairs[:, j, :, e],
-                        scalar=decay[:, PAIR * j + e : PAIR * j + e + 1],
-                        in1=kv_of[j][:, e, :],
-                        op0=MULT,
-                        op1=ADD,
-                    )
-                if u == PAIR - 1:
-                    h_grouped = work.tile([P, TOKENS, PACK], BF16, align_bytes=64)
-                    nc.vector.tensor_tensor(
-                        out=h_grouped[:],
-                        in0=gate[:].rearrange("p t k -> p k t"),
-                        in1=new_state_t[:].rearrange("p t k -> p k t"),
-                        op=MULT,
-                    )
-                    cols = slice(g * TOKENS, (g + 1) * TOKENS)
-                    nc.vector.quantize_mx(
-                        out=h_codes[:, cols].bitcast(FP8X4),
-                        scales=h_scales[:, cols],
-                        in_=h_grouped[:].rearrange("p k t -> p (k t)"),
-                    )
+                h_of[g] = work.tile([P, TOKENS, PACK], BF16, align_bytes=64, name="h_grouped")
+                nc.vector.tensor_tensor(
+                    out=h_of[g][:],
+                    in0=gate_of[g][:].rearrange("p t k -> p k t"),
+                    in1=new_state_of[g][:].rearrange("p t k -> p k t"),
+                    op=MULT,
+                )
+
+        def end_on_vector(i):
+            w, g = steps[i]
+            if w == VALUE:
+                for u in range(PAIR):
+                    for e in range(PAIR):
+                        j = PAIR * g + u
+                        nc.vector.scalar_tensor_tensor(
+                            out=new_state_of[g][:, PAIR * u + e, :],
+                            in0=state_pairs[:, j, :, e],
+                            scalar=decay[:, PAIR * j + e : PAIR * j + e + 1],
+                            in1=new_state_of[g][:, PAIR * u + e, :],
+                            op0=MULT,
+                            op1=ADD,
+                        )
+            elif w == RECEPTANCE:
+                nc.vector.quantize_mx(
+                    out=h_codes[:, token_columns(g)].bitcast(FP8X4),
+                    scales=h_scales[:, token_columns(g)],
+                    in_=h_of[g][:].rearrange("p k t -> p (k t)"),
+                )
 
         def return_new_state(g):
-            new_state_t = per_pass[g][1]
             bank = banks.tile([P, BANK], F32, tag="bank")
             for value in range(PACK):
-                nc.tensor.transpose(bank[:, value * P : (value + 1) * P], new_state_t[:, value, :], ident[:])
+                nc.tensor.transpose(bank[:, value * P : (value + 1) * P], new_state_of[g][:, value, :], ident[:])
             natural = stores.tile([P, BANK], F32)
             nc.scalar.copy(
                 out=natural[:].rearrange("k (u c e) -> k u c e", u=PAIR, e=PAIR),
@@ -294,27 +307,35 @@ def tile_rwkvtimemix_pa_kernel(tc, x, state, Wk, Wv, Wr, Wo, time_decay, time_cu
             )
             return natural
 
-        multiply_order = list(range(first_out_unit)) + [None] + list(range(first_out_unit, len(units)))
-        units_of_a_pass = 3 * PAIR
+        first_out_step = steps.index((OUTPUT, 0))
+        multiplied_in = {}
+        for i in range(len(steps)):
+            multiplied_in.setdefault(i + 2 if i == first_out_step else i + 1, []).append(i)
         returned = []
-        for i in range(len(multiply_order) + FINISH_AFTER):
-            if i + LOAD_AHEAD < len(units):
-                load_unit(i + LOAD_AHEAD)
-            finishing = multiply_order[i - FINISH_AFTER] if i >= FINISH_AFTER else None
-            if finishing is not None:
-                finish_on_scalar(finishing)
-            if i < len(units):
-                transpose(i)
-            if 0 <= i - QUANTISE_AFTER < len(units):
-                quantise(i - QUANTISE_AFTER)
-            if finishing is not None:
-                finish_on_vector(finishing)
-            n = i - RETURN_AFTER
-            if 0 <= n < first_out_unit and n % units_of_a_pass == units_of_a_pass - 1:
-                returned.append((n // units_of_a_pass, return_new_state(n // units_of_a_pass)))
-            if i + LOAD_AHEAD >= len(units) - 1:
+        for i in range(len(steps) + 3):
+            for n in range(STEP_UNITS * i + LOAD_AHEAD, STEP_UNITS * (i + 1) + LOAD_AHEAD):
+                if n < len(units):
+                    load_unit(n)
+            finishing = multiplied_in.get(i - 1, [])
+            for done in finishing:
+                finish_on_scalar(done)
+            if i < len(steps):
+                transpose(STEP_UNITS * i)
+            if 0 < i <= len(steps):
+                quantise(STEP_UNITS * i - 1)
+            for done in finishing:
+                begin_on_vector(done)
+            if i < len(steps):
+                transpose(STEP_UNITS * i + 1)
+                quantise(STEP_UNITS * i)
+            for done in finishing:
+                end_on_vector(done)
+            for done in multiplied_in.get(i - 2, []):
+                if steps[done][0] == VALUE:
+                    returned.append((steps[done][1], return_new_state(steps[done][1])))
+            if STEP_UNITS * (i + 1) + LOAD_AHEAD >= len(units):
                 for g, natural in returned:
                     nc.sync.dma_start(out=new_state_rows[:, g * BANK : (g + 1) * BANK], in_=natural[:])
                 returned = []
-            if 0 <= i - MULTIPLY_AFTER < len(multiply_order) and multiply_order[i - MULTIPLY_AFTER] is not None:
-                multiply(multiply_order[i - MULTIPLY_AFTER])
+            for ready in multiplied_in.get(i, []):
+                multiply(ready)

@@ -10,6 +10,7 @@ U8 = mybir.dt.uint8
 FP8X4 = mybir.dt.float8_e4m3fn_x4
 MULT = mybir.AluOpType.mult
 ADD = mybir.AluOpType.add
+SUB = mybir.AluOpType.subtract
 ACT = mybir.ActivationFunctionType
 
 P = 128
@@ -27,6 +28,7 @@ CHUNK_BANKS = ROW_WORDS // BANK
 RAW_BUFS = 12
 STEP_UNITS = 2
 LOAD_AHEAD = RAW_BUFS - STEP_UNITS
+STATE_AFTER = 4
 VECTOR_JOINS_AT = 3
 KEY = 0
 VALUE = 1
@@ -75,13 +77,15 @@ def tile_rwkvtimemix_pa_kernel(tc, x, state, Wk, Wv, Wr, Wo, time_decay, time_cu
             out=shift[:].rearrange("p (b t) -> p b t", t=SEQ_LEN)[:, :, 1:SEQ_LEN],
             in_=ident[:].rearrange("p (b t) -> p b t", t=SEQ_LEN)[:, :, 0 : SEQ_LEN - 1],
         )
+        step = keep.tile([P, P], BF16)
+        nc.vector.tensor_tensor(out=step[:], in0=ident[:], in1=shift[:], op=SUB)
 
         state_sb = keep.tile([P, CHANNELS], BF16)
-        nc.sync.dma_start(out=state_sb[:], in_=state.rearrange("b t d -> (b t) d"))
-
         raw_words = {}
 
         def load_unit(n):
+            if n == STATE_AFTER:
+                nc.sync.dma_start(out=state_sb[:], in_=state.rearrange("b t d -> (b t) d"))
             w, j = units[n]
             raw = raw_pool.tile([P, PAIR * CHANNELS], BF16)
             unit_rows = weights[w][j * P * PAIR : (j + 1) * P * PAIR, :]
@@ -105,46 +109,44 @@ def tile_rwkvtimemix_pa_kernel(tc, x, state, Wk, Wv, Wr, Wo, time_decay, time_cu
         per_channel = keep.tile([P, 2 * UNITS * PAIR], F32)
         nc.vector.tensor_copy(out=per_channel[:], in_=bank[:].bitcast(BF16)[:, 0 : 2 * UNITS * PAIR])
         curve = per_channel[:, 0 : UNITS * PAIR]
-        one_minus_curve = keep.tile([P, UNITS * PAIR], F32)
-        nc.vector.tensor_scalar(out=one_minus_curve[:], in0=curve, scalar1=-1.0, scalar2=1.0, op0=MULT, op1=ADD)
         exp_decay = keep.tile([P, UNITS * PAIR], F32)
         nc.scalar.activation(out=exp_decay[:], in_=per_channel[:, UNITS * PAIR : 2 * UNITS * PAIR], func=ACT.Exp)
         decay = keep.tile([P, UNITS * PAIR], F32)
         nc.scalar.activation(out=decay[:], in_=exp_decay[:], func=ACT.Exp, scale=-1.0)
 
-        def over_tokens(columns, four_j):
-            pairs = columns.rearrange("p (j e) -> p j e", e=PAIR)[:, four_j, :]
-            return pairs.unsqueeze(2).to_broadcast([P, BANK_BLOCKS, TOKENS, PAIR])
-
         x_words = x_sb[:].bitcast(F32)
-        now_part = keep.tile([P, UNITS, TOKENS, PAIR], F32)
-        before_part = keep.tile([P, UNITS, TOKENS, PAIR], F32)
+        x_pairs = x_sb[:].rearrange("k (j c e) -> k j c e", j=UNITS, e=PAIR)
         xm_grouped = keep.tile([P, PASSES, TOKENS, PACK], BF16, align_bytes=64)
-        for half in range(UNITS // BANK_BLOCKS):
-            four_j = slice(half * BANK_BLOCKS, (half + 1) * BANK_BLOCKS)
-            now = banks.tile([P, BANK], F32, tag="bank")
+        for half in range(PASSES // PAIR):
             before = banks.tile([P, BANK], F32, tag="bank")
-            for target, mover in ((now, ident), (before, shift)):
-                for q in range(BANK_BLOCKS):
-                    j = half * BANK_BLOCKS + q
-                    nc.tensor.transpose(target[:, q * P : (q + 1) * P], x_words[:, j * P : (j + 1) * P], mover[:])
-            nc.vector.tensor_tensor(
-                out=now_part[:, four_j, :, :],
-                in0=now[:].bitcast(BF16).rearrange("p (j k e) -> p j k e", j=BANK_BLOCKS, e=PAIR),
-                in1=over_tokens(curve, four_j),
-                op=MULT,
-            )
-            nc.vector.tensor_tensor(
-                out=before_part[:, four_j, :, :],
-                in0=before[:].bitcast(BF16).rearrange("p (j k e) -> p j k e", j=BANK_BLOCKS, e=PAIR),
-                in1=over_tokens(one_minus_curve[:], four_j),
-                op=MULT,
-            )
-            for g in range(half * BANK_BLOCKS // PAIR, (half + 1) * BANK_BLOCKS // PAIR):
+            for q in range(BANK_BLOCKS):
+                j = half * BANK_BLOCKS + q
+                nc.tensor.transpose(before[:, q * P : (q + 1) * P], x_words[:, j * P : (j + 1) * P], shift[:])
+            before_pairs = before[:].bitcast(BF16).rearrange("p (g u k e) -> p g k u e", g=PAIR, u=PAIR, e=PAIR)
+            for q in range(PAIR):
+                g = half * PAIR + q
+                change = banks.tile([P, BANK], F32, tag="bank")
+                for u in range(PAIR):
+                    for e in range(PAIR):
+                        value = PAIR * u + e
+                        nc.tensor.matmul(
+                            out=change[:, value * P : (value + 1) * P],
+                            lhsT=x_pairs[:, PAIR * g + u, :, e],
+                            rhs=step[:],
+                            start=True,
+                            stop=True,
+                        )
+                scaled = work.tile([P, PACK, TOKENS], F32)
+                nc.vector.tensor_tensor(
+                    out=scaled[:],
+                    in0=change[:].rearrange("p (t k) -> p t k", t=PACK),
+                    in1=curve[:, PACK * g : PACK * (g + 1)].unsqueeze(2).to_broadcast([P, PACK, TOKENS]),
+                    op=MULT,
+                )
                 nc.vector.tensor_tensor(
                     out=xm_grouped[:, g, :, :].rearrange("p k (u e) -> p k u e", e=PAIR),
-                    in0=now_part[:, PAIR * g : PAIR * g + PAIR, :, :].rearrange("p u k e -> p k u e"),
-                    in1=before_part[:, PAIR * g : PAIR * g + PAIR, :, :].rearrange("p u k e -> p k u e"),
+                    in0=before_pairs[:, q, :, :, :],
+                    in1=scaled[:].rearrange("p (u e) k -> p k u e", e=PAIR),
                     op=ADD,
                 )
         xm_codes = keep.tile([P, PASSES * TOKENS], U32, align_bytes=64)
@@ -156,14 +158,6 @@ def tile_rwkvtimemix_pa_kernel(tc, x, state, Wk, Wv, Wr, Wo, time_decay, time_cu
         )
 
         state_words = state_sb[:].bitcast(F32)
-        state_t = keep.tile([P, UNITS * TOKENS], F32)
-        for half in range(UNITS // BANK_BLOCKS):
-            bank = banks.tile([P, BANK], F32, tag="bank")
-            for q in range(BANK_BLOCKS):
-                j = half * BANK_BLOCKS + q
-                nc.tensor.transpose(bank[:, q * P : (q + 1) * P], state_words[:, j * P : (j + 1) * P], ident[:])
-            nc.scalar.copy(out=state_t[:, half * BANK : (half + 1) * BANK], in_=bank[:])
-        state_pairs = state_t[:].bitcast(BF16).rearrange("p (j k e) -> p j k e", j=UNITS, e=PAIR)
 
         h_codes = keep.tile([P, PASSES * TOKENS], U32, align_bytes=64)
         h_scales = keep.tile([P, PASSES * TOKENS], U8, align_bytes=64)
@@ -278,12 +272,17 @@ def tile_rwkvtimemix_pa_kernel(tc, x, state, Wk, Wv, Wr, Wo, time_decay, time_cu
         def end_on_vector(i):
             w, g = steps[i]
             if w == VALUE:
+                bank = banks.tile([P, BANK], F32, tag="bank")
+                for u in range(PAIR):
+                    j = PAIR * g + u
+                    nc.tensor.transpose(bank[:, u * P : (u + 1) * P], state_words[:, j * P : (j + 1) * P], ident[:])
+                state_pairs = bank[:].bitcast(BF16)[:, 0 : PAIR * TOKENS * PAIR].rearrange("p (u k e) -> p u k e", u=PAIR, e=PAIR)
                 for u in range(PAIR):
                     for e in range(PAIR):
                         j = PAIR * g + u
                         nc.vector.scalar_tensor_tensor(
                             out=new_state_of[g][:, PAIR * u + e, :],
-                            in0=state_pairs[:, j, :, e],
+                            in0=state_pairs[:, u, :, e],
                             scalar=decay[:, PAIR * j + e : PAIR * j + e + 1],
                             in1=new_state_of[g][:, PAIR * u + e, :],
                             op0=MULT,

@@ -25,10 +25,10 @@ ROW_WORDS = CHANNELS // PAIR
 BANK = 512
 BANK_BLOCKS = BANK // P
 CHUNK_BANKS = ROW_WORDS // BANK
-RAW_BUFS = 12
 STEP_UNITS = 2
-LOAD_AHEAD = RAW_BUFS - STEP_UNITS
-STATE_AFTER = 4
+RAW_BUFS = 6
+LOAD_AHEAD = RAW_BUFS - 1
+STATE_AFTER = 2
 VECTOR_JOINS_AT = 3
 KEY = 0
 VALUE = 1
@@ -49,7 +49,8 @@ def tile_rwkvtimemix_pa_kernel(tc, x, state, Wk, Wv, Wr, Wo, time_decay, time_cu
         steps.extend([(KEY, g), (VALUE, g), (RECEPTANCE, g)])
     for g in range(PASSES):
         steps.append((OUTPUT, g))
-    units = [(w, STEP_UNITS * g + u) for w, g in steps for u in range(STEP_UNITS)]
+    first_out_unit = STEP_UNITS * steps.index((OUTPUT, 0))
+    last_unit = STEP_UNITS * len(steps) - 1
 
     with ExitStack() as ctx:
         ctx.enter_context(tc.manual_schedule())
@@ -58,7 +59,7 @@ def tile_rwkvtimemix_pa_kernel(tc, x, state, Wk, Wv, Wr, Wo, time_decay, time_cu
         grouped_pool = ctx.enter_context(tc.tile_pool(name="grouped", bufs=4))
         codes_pool = ctx.enter_context(tc.tile_pool(name="codes", bufs=3 * STEP_UNITS))
         work = ctx.enter_context(tc.tile_pool(name="work", bufs=2))
-        stores = ctx.enter_context(tc.tile_pool(name="stores", bufs=4))
+        stores = ctx.enter_context(tc.tile_pool(name="stores", bufs=8))
         banks = ctx.enter_context(tc.psum_pool(name="banks", bufs=6))
         sums = ctx.enter_context(tc.psum_pool(name="sums", bufs=2))
 
@@ -83,26 +84,23 @@ def tile_rwkvtimemix_pa_kernel(tc, x, state, Wk, Wv, Wr, Wo, time_decay, time_cu
         state_sb = keep.tile([P, CHANNELS], BF16)
         raw_words = {}
 
-        def load_unit(n):
-            if n == STATE_AFTER:
+        def load_step(i):
+            if i == STATE_AFTER:
                 nc.sync.dma_start(out=state_sb[:], in_=state.rearrange("b t d -> (b t) d"))
-            w, j = units[n]
-            raw = raw_pool.tile([P, PAIR * CHANNELS], BF16)
-            unit_rows = weights[w][j * P * PAIR : (j + 1) * P * PAIR, :]
-            if n < len(units) - 1:
-                nc.sync.dma_start(out=raw[:], in_=unit_rows.rearrange("(p e) k -> p (e k)", e=PAIR))
+            w, g = steps[i]
+            raw = raw_pool.tile([P, STEP_UNITS, PAIR, CHANNELS], BF16)
+            rows = weights[w][g * BANK : (g + 1) * BANK, :].rearrange("(u p e) k -> p u e k", u=STEP_UNITS, e=PAIR)
+            if i < len(steps) - 1:
+                pieces = [(u, slice(0, CHANNELS)) for u in range(STEP_UNITS)]
             else:
-                half_row = CHANNELS // CHUNK_BANKS
-                for half in range(CHUNK_BANKS):
-                    cols = slice(half * half_row, (half + 1) * half_row)
-                    nc.sync.dma_start(
-                        out=raw[:].rearrange("p (e k) -> p e k", e=PAIR)[:, :, cols],
-                        in_=unit_rows.rearrange("(p e) k -> p e k", e=PAIR)[:, :, cols],
-                    )
-            raw_words[n] = raw[:].bitcast(F32)
+                pieces = [(0, slice(0, CHANNELS)), (1, slice(0, CHANNELS // 2)), (1, slice(CHANNELS // 2, CHANNELS))]
+            for u, cols in pieces:
+                nc.sync.dma_start(out=raw[:, u, :, cols], in_=rows[:, u, :, cols])
+            for u in range(STEP_UNITS):
+                raw_words[STEP_UNITS * i + u] = raw[:, u, :, :].rearrange("p e k -> p (e k)").bitcast(F32)
 
-        for n in range(LOAD_AHEAD):
-            load_unit(n)
+        for i in range(LOAD_AHEAD):
+            load_step(i)
 
         bank = banks.tile([P, BANK], F32, tag="bank")
         nc.tensor.transpose(bank[:, 0:P], vectors[:].bitcast(F32), ident[:])
@@ -165,10 +163,16 @@ def tile_rwkvtimemix_pa_kernel(tc, x, state, Wk, Wv, Wr, Wo, time_decay, time_cu
         grouped_of = {}
         quantised = {}
         sums_of = {}
+        out_sums_of = {}
         k_of = {}
         new_state_of = {}
         gate_of = {}
         h_of = {}
+
+        def vector_bank(n):
+            if n < VECTOR_JOINS_AT:
+                return None
+            return (1, 0) if n == last_unit else (0, 0)
 
         def transpose(n):
             grouped = grouped_pool.tile([P, PASSES * PAIR * P * PACK], BF16, align_bytes=64)
@@ -181,7 +185,7 @@ def tile_rwkvtimemix_pa_kernel(tc, x, state, Wk, Wv, Wr, Wo, time_decay, time_cu
                         nc.tensor.transpose(bank[:, q * P : (q + 1) * P], raw_words[n][:, first : first + P], ident[:])
                     source = bank[:].rearrange("p (g u c) -> p g c u", g=PAIR, u=PAIR)
                     target = grouped_words[:, PAIR * half : PAIR * half + PAIR, e, :, :]
-                    if e == 0 and half == 0 and n >= VECTOR_JOINS_AT:
+                    if (half, e) == vector_bank(n):
                         nc.vector.tensor_copy(out=target, in_=source)
                     else:
                         nc.scalar.copy(out=target, in_=source)
@@ -221,23 +225,29 @@ def tile_rwkvtimemix_pa_kernel(tc, x, state, Wk, Wv, Wr, Wo, time_decay, time_cu
             return lambda g: slice((g * PAIR + e) * P, (g * PAIR + e + 1) * P)
 
         def multiply(i):
-            w, g = steps[i]
             sums_of[i] = sums.tile([P, PACK, TOKENS], F32, tag="sum", name="products")
             for u in range(STEP_UNITS):
                 codes, scales = quantised[STEP_UNITS * i + u]
-                if w == OUTPUT:
+                for e in range(PAIR):
                     contract(
-                        sums_of[i][:, PAIR * u : PAIR * u + PAIR, :].rearrange("k e c -> k (e c)"),
-                        (h_codes, h_scales, token_columns),
-                        (codes, scales, unit_columns),
+                        sums_of[i][:, PAIR * u + e, :],
+                        (codes, scales, chunk_columns(e)),
+                        (xm_codes, xm_scales, token_columns),
                     )
-                else:
-                    for e in range(PAIR):
-                        contract(
-                            sums_of[i][:, PAIR * u + e, :],
-                            (codes, scales, chunk_columns(e)),
-                            (xm_codes, xm_scales, token_columns),
-                        )
+
+        def multiply_out(n):
+            codes, scales = quantised[n]
+            out_sums_of[n] = sums.tile([P, PAIR * P], F32, tag="sum", name="out_sums")
+            contract(out_sums_of[n][:], (h_codes, h_scales, token_columns), (codes, scales, unit_columns))
+
+        def store_out(n):
+            j = n - first_out_unit
+            out_sb = stores.tile([P, PAIR * P], F32)
+            nc.scalar.copy(
+                out=out_sb[:].rearrange("k (c e) -> k c e", e=PAIR),
+                in_=out_sums_of[n][:].rearrange("k (e c) -> k c e", e=PAIR),
+            )
+            nc.sync.dma_start(out=out_rows[:, j * PAIR * P : (j + 1) * PAIR * P], in_=out_sb[:])
 
         def finish_on_scalar(i):
             w, g = steps[i]
@@ -247,13 +257,6 @@ def tile_rwkvtimemix_pa_kernel(tc, x, state, Wk, Wv, Wr, Wo, time_decay, time_cu
             elif w == RECEPTANCE:
                 gate_of[g] = work.tile([P, PACK, TOKENS], F32, name="gate")
                 nc.scalar.activation(out=gate_of[g][:], in_=sums_of[i][:], func=ACT.Sigmoid)
-            elif w == OUTPUT:
-                out_sb = stores.tile([P, BANK], F32)
-                nc.scalar.copy(
-                    out=out_sb[:].rearrange("k (u c e) -> k u c e", u=PAIR, e=PAIR),
-                    in_=sums_of[i][:].rearrange("k (u e) c -> k u c e", u=PAIR),
-                )
-                nc.sync.dma_start(out=out_rows[:, g * BANK : (g + 1) * BANK], in_=out_sb[:])
 
         def begin_on_vector(i):
             w, g = steps[i]
@@ -306,35 +309,59 @@ def tile_rwkvtimemix_pa_kernel(tc, x, state, Wk, Wv, Wr, Wo, time_decay, time_cu
             )
             return natural
 
-        first_out_step = steps.index((OUTPUT, 0))
-        multiplied_in = {}
-        for i in range(len(steps)):
-            multiplied_in.setdefault(i + 2 if i == first_out_step else i + 1, []).append(i)
         returned = []
-        for i in range(len(steps) + 3):
-            for n in range(STEP_UNITS * i + LOAD_AHEAD, STEP_UNITS * (i + 1) + LOAD_AHEAD):
-                if n < len(units):
-                    load_unit(n)
-            finishing = multiplied_in.get(i - 1, [])
-            for done in finishing:
-                finish_on_scalar(done)
-            if i < len(steps):
-                transpose(STEP_UNITS * i)
-            if 0 < i <= len(steps):
+
+        def store_returned():
+            for g, natural in returned:
+                nc.sync.dma_start(out=new_state_rows[:, g * BANK : (g + 1) * BANK], in_=natural[:])
+            returned.clear()
+
+        out_step = steps.index((OUTPUT, 0))
+        for i in range(out_step):
+            if i + LOAD_AHEAD < len(steps):
+                load_step(i + LOAD_AHEAD)
+            if i >= 2:
+                finish_on_scalar(i - 2)
+            transpose(STEP_UNITS * i)
+            if i >= 1:
                 quantise(STEP_UNITS * i - 1)
-            for done in finishing:
-                begin_on_vector(done)
-            if i < len(steps):
-                transpose(STEP_UNITS * i + 1)
-                quantise(STEP_UNITS * i)
-            for done in finishing:
-                end_on_vector(done)
-            for done in multiplied_in.get(i - 2, []):
-                if steps[done][0] == VALUE:
-                    returned.append((steps[done][1], return_new_state(steps[done][1])))
-            if STEP_UNITS * (i + 1) + LOAD_AHEAD >= len(units):
-                for g, natural in returned:
-                    nc.sync.dma_start(out=new_state_rows[:, g * BANK : (g + 1) * BANK], in_=natural[:])
-                returned = []
-            for ready in multiplied_in.get(i, []):
-                multiply(ready)
+            if i >= 2:
+                begin_on_vector(i - 2)
+            transpose(STEP_UNITS * i + 1)
+            quantise(STEP_UNITS * i)
+            if i >= 2:
+                end_on_vector(i - 2)
+            if i >= 3 and steps[i - 3][0] == VALUE:
+                returned.append((steps[i - 3][1], return_new_state(steps[i - 3][1])))
+            if i + LOAD_AHEAD >= len(steps) - 1:
+                store_returned()
+            if i >= 1:
+                multiply(i - 1)
+
+        value_step, gate_step = out_step - 2, out_step - 1
+        ready = first_out_unit
+        for n in range(first_out_unit, last_unit + 1):
+            if n == first_out_unit + 1:
+                finish_on_scalar(gate_step)
+            transpose(n)
+            if n == first_out_unit:
+                quantise(n - 1)
+                begin_on_vector(value_step)
+                multiply(gate_step)
+                end_on_vector(value_step)
+            elif n == first_out_unit + 1:
+                begin_on_vector(gate_step)
+                returned.append((PASSES - 1, return_new_state(PASSES - 1)))
+                store_returned()
+            quantise(n)
+            if n == first_out_unit + 1:
+                end_on_vector(gate_step)
+            elif n > first_out_unit + 1:
+                while ready < n - 2:
+                    multiply_out(ready)
+                    store_out(ready)
+                    ready += 1
+        while ready <= last_unit:
+            multiply_out(ready)
+            store_out(ready)
+            ready += 1

@@ -29,7 +29,9 @@ STEP_UNITS = 2
 RAW_BUFS = 6
 LOAD_AHEAD = RAW_BUFS - 1
 STATE_AFTER = 2
-VECTOR_JOINS_AT = 3
+MULTIPLY_AFTER = 2
+MULTIPLY_OUT_AFTER = 4
+VECTOR_JOINS_AT = 2
 KEY = 0
 VALUE = 1
 RECEPTANCE = 2
@@ -57,7 +59,7 @@ def tile_rwkvtimemix_pa_kernel(tc, x, state, Wk, Wv, Wr, Wo, time_decay, time_cu
         keep = ctx.enter_context(tc.tile_pool(name="keep", bufs=1))
         raw_pool = ctx.enter_context(tc.tile_pool(name="raw", bufs=RAW_BUFS))
         grouped_pool = ctx.enter_context(tc.tile_pool(name="grouped", bufs=4))
-        codes_pool = ctx.enter_context(tc.tile_pool(name="codes", bufs=3 * STEP_UNITS))
+        codes_pool = ctx.enter_context(tc.tile_pool(name="codes", bufs=MULTIPLY_OUT_AFTER + 1))
         work = ctx.enter_context(tc.tile_pool(name="work", bufs=2))
         stores = ctx.enter_context(tc.tile_pool(name="stores", bufs=8))
         banks = ctx.enter_context(tc.psum_pool(name="banks", bufs=6))
@@ -111,6 +113,8 @@ def tile_rwkvtimemix_pa_kernel(tc, x, state, Wk, Wv, Wr, Wo, time_decay, time_cu
         nc.scalar.activation(out=exp_decay[:], in_=per_channel[:, UNITS * PAIR : 2 * UNITS * PAIR], func=ACT.Exp)
         decay = keep.tile([P, UNITS * PAIR], F32)
         nc.scalar.activation(out=decay[:], in_=exp_decay[:], func=ACT.Exp, scale=-1.0)
+        table_loader = keep.tile([P, 1], F32)
+        nc.scalar.activation(out=table_loader[:], in_=decay[:, 0:1], func=ACT.Sigmoid)
 
         x_words = x_sb[:].bitcast(F32)
         x_pairs = x_sb[:].rearrange("k (j c e) -> k j c e", j=UNITS, e=PAIR)
@@ -123,7 +127,7 @@ def tile_rwkvtimemix_pa_kernel(tc, x, state, Wk, Wv, Wr, Wo, time_decay, time_cu
             before_pairs = before[:].bitcast(BF16).rearrange("p (g u k e) -> p g k u e", g=PAIR, u=PAIR, e=PAIR)
             for q in range(PAIR):
                 g = half * PAIR + q
-                change = banks.tile([P, BANK], F32, tag="bank")
+                change = sums.tile([P, BANK], F32, tag="sum")
                 for u in range(PAIR):
                     for e in range(PAIR):
                         value = PAIR * u + e
@@ -169,11 +173,6 @@ def tile_rwkvtimemix_pa_kernel(tc, x, state, Wk, Wv, Wr, Wo, time_decay, time_cu
         gate_of = {}
         h_of = {}
 
-        def vector_bank(n):
-            if n < VECTOR_JOINS_AT:
-                return None
-            return (1, 0) if n == last_unit else (0, 0)
-
         def transpose(n):
             grouped = grouped_pool.tile([P, PASSES * PAIR * P * PACK], BF16, align_bytes=64)
             grouped_words = grouped[:].bitcast(F32).rearrange("p (g e c u) -> p g e c u", g=PASSES, e=PAIR, u=PAIR)
@@ -185,7 +184,7 @@ def tile_rwkvtimemix_pa_kernel(tc, x, state, Wk, Wv, Wr, Wo, time_decay, time_cu
                         nc.tensor.transpose(bank[:, q * P : (q + 1) * P], raw_words[n][:, first : first + P], ident[:])
                     source = bank[:].rearrange("p (g u c) -> p g c u", g=PAIR, u=PAIR)
                     target = grouped_words[:, PAIR * half : PAIR * half + PAIR, e, :, :]
-                    if (half, e) == vector_bank(n):
+                    if n >= VECTOR_JOINS_AT and half == CHUNK_BANKS - 1 and e == PAIR - 1:
                         nc.vector.tensor_copy(out=target, in_=source)
                     else:
                         nc.scalar.copy(out=target, in_=source)
@@ -224,16 +223,17 @@ def tile_rwkvtimemix_pa_kernel(tc, x, state, Wk, Wv, Wr, Wo, time_decay, time_cu
         def chunk_columns(e):
             return lambda g: slice((g * PAIR + e) * P, (g * PAIR + e + 1) * P)
 
-        def multiply(i):
-            sums_of[i] = sums.tile([P, PACK, TOKENS], F32, tag="sum", name="products")
-            for u in range(STEP_UNITS):
-                codes, scales = quantised[STEP_UNITS * i + u]
-                for e in range(PAIR):
-                    contract(
-                        sums_of[i][:, PAIR * u + e, :],
-                        (codes, scales, chunk_columns(e)),
-                        (xm_codes, xm_scales, token_columns),
-                    )
+        def multiply(n):
+            i, u = divmod(n, STEP_UNITS)
+            if u == 0:
+                sums_of[i] = sums.tile([P, PACK, TOKENS], F32, tag="sum", name="products")
+            codes, scales = quantised[n]
+            for e in range(PAIR):
+                contract(
+                    sums_of[i][:, PAIR * u + e, :],
+                    (codes, scales, chunk_columns(e)),
+                    (xm_codes, xm_scales, token_columns),
+                )
 
         def multiply_out(n):
             codes, scales = quantised[n]
@@ -316,52 +316,31 @@ def tile_rwkvtimemix_pa_kernel(tc, x, state, Wk, Wv, Wr, Wo, time_decay, time_cu
                 nc.sync.dma_start(out=new_state_rows[:, g * BANK : (g + 1) * BANK], in_=natural[:])
             returned.clear()
 
-        out_step = steps.index((OUTPUT, 0))
-        for i in range(out_step):
-            if i + LOAD_AHEAD < len(steps):
+        for n in range(last_unit + 1):
+            i, u = divmod(n, STEP_UNITS)
+            if u == 0 and i + LOAD_AHEAD < len(steps):
                 load_step(i + LOAD_AHEAD)
-            if i >= 2:
-                finish_on_scalar(i - 2)
-            transpose(STEP_UNITS * i)
-            if i >= 1:
-                quantise(STEP_UNITS * i - 1)
-            if i >= 2:
-                begin_on_vector(i - 2)
-            transpose(STEP_UNITS * i + 1)
-            quantise(STEP_UNITS * i)
-            if i >= 2:
-                end_on_vector(i - 2)
-            if i >= 3 and steps[i - 3][0] == VALUE:
-                returned.append((steps[i - 3][1], return_new_state(steps[i - 3][1])))
+            finishing = i - STEP_UNITS if 0 <= STEP_UNITS * (i - STEP_UNITS) < first_out_unit else None
+            if u == 0 and finishing is not None:
+                finish_on_scalar(finishing)
+            if n > 0:
+                quantise(n - 1)
+            transpose(n)
+            if finishing is not None:
+                if u == 0:
+                    begin_on_vector(finishing)
+                else:
+                    end_on_vector(finishing)
+                    if steps[finishing][0] == RECEPTANCE:
+                        returned.append((steps[finishing][1], return_new_state(steps[finishing][1])))
             if i + LOAD_AHEAD >= len(steps) - 1:
                 store_returned()
-            if i >= 1:
-                multiply(i - 1)
-
-        value_step, gate_step = out_step - 2, out_step - 1
-        ready = first_out_unit
-        for n in range(first_out_unit, last_unit + 1):
-            if n == first_out_unit + 1:
-                finish_on_scalar(gate_step)
-            transpose(n)
-            if n == first_out_unit:
-                quantise(n - 1)
-                begin_on_vector(value_step)
-                multiply(gate_step)
-                end_on_vector(value_step)
-            elif n == first_out_unit + 1:
-                begin_on_vector(gate_step)
-                returned.append((PASSES - 1, return_new_state(PASSES - 1)))
-                store_returned()
-            quantise(n)
-            if n == first_out_unit + 1:
-                end_on_vector(gate_step)
-            elif n > first_out_unit + 1:
-                while ready < n - 2:
-                    multiply_out(ready)
-                    store_out(ready)
-                    ready += 1
-        while ready <= last_unit:
-            multiply_out(ready)
-            store_out(ready)
-            ready += 1
+            if 0 <= n - MULTIPLY_AFTER < first_out_unit:
+                multiply(n - MULTIPLY_AFTER)
+            if n - MULTIPLY_OUT_AFTER >= first_out_unit:
+                multiply_out(n - MULTIPLY_OUT_AFTER)
+                store_out(n - MULTIPLY_OUT_AFTER)
+        quantise(last_unit)
+        for n in range(last_unit - MULTIPLY_OUT_AFTER + 1, last_unit + 1):
+            multiply_out(n)
+            store_out(n)

@@ -92,10 +92,11 @@ def tile_rwkvtimemix_pa_kernel(tc, x, state, Wk, Wv, Wr, Wo, time_decay, time_cu
             w, g = steps[i]
             raw = raw_pool.tile([P, STEP_UNITS, PAIR, CHANNELS], BF16)
             rows = weights[w][g * BANK : (g + 1) * BANK, :].rearrange("(u p e) k -> p u e k", u=STEP_UNITS, e=PAIR)
-            if i < len(steps) - 1:
-                pieces = [(u, slice(0, CHANNELS)) for u in range(STEP_UNITS)]
+            if i < len(steps) - 2:
+                halves = [slice(0, CHANNELS)]
             else:
-                pieces = [(0, slice(0, CHANNELS)), (1, slice(0, CHANNELS // 2)), (1, slice(CHANNELS // 2, CHANNELS))]
+                halves = [slice(0, CHANNELS // 2), slice(CHANNELS // 2, CHANNELS)]
+            pieces = [(u, cols) for u in range(STEP_UNITS) for cols in halves]
             for u, cols in pieces:
                 nc.sync.dma_start(out=raw[:, u, :, cols], in_=rows[:, u, :, cols])
             for u in range(STEP_UNITS):
@@ -237,7 +238,10 @@ def tile_rwkvtimemix_pa_kernel(tc, x, state, Wk, Wv, Wr, Wo, time_decay, time_cu
 
         def multiply_out(n):
             codes, scales = quantised[n]
-            out_sums_of[n] = sums.tile([P, PAIR * P], F32, tag="sum", name="out_sums")
+            if n > last_unit - MULTIPLY_OUT_AFTER:
+                out_sums_of[n] = banks.tile([P, PAIR * P], F32, tag="bank", name="out_sums")
+            else:
+                out_sums_of[n] = sums.tile([P, PAIR * P], F32, tag="sum", name="out_sums")
             contract(out_sums_of[n][:], (h_codes, h_scales, token_columns), (codes, scales, unit_columns))
 
         def store_out(n):

@@ -61,7 +61,6 @@ def tile_rwkvtimemix_pa_kernel(tc, x, state, Wk, Wv, Wr, Wo, time_decay, time_cu
         grouped_pool = ctx.enter_context(tc.tile_pool(name="grouped", bufs=4))
         codes_pool = ctx.enter_context(tc.tile_pool(name="codes", bufs=MULTIPLY_OUT_AFTER + 1))
         work = ctx.enter_context(tc.tile_pool(name="work", bufs=2))
-        stores = ctx.enter_context(tc.tile_pool(name="stores", bufs=8))
         banks = ctx.enter_context(tc.psum_pool(name="banks", bufs=6))
         sums = ctx.enter_context(tc.psum_pool(name="sums", bufs=2))
 
@@ -168,6 +167,15 @@ def tile_rwkvtimemix_pa_kernel(tc, x, state, Wk, Wv, Wr, Wo, time_decay, time_cu
         grouped_of = {}
         quantised = {}
         sums_of = {}
+        store_of = {}
+        first = first_out_unit
+        while first <= last_unit:
+            count = max(1, (last_unit + 1 - first) // 2)
+            for n in range(first, first + count):
+                store_of[n] = (first, count)
+            first += count
+        out_sb_of = {}
+        new_state_sb = keep.tile([P, CHANNELS], F32)
         out_sums_of = {}
         k_of = {}
         new_state_of = {}
@@ -245,13 +253,17 @@ def tile_rwkvtimemix_pa_kernel(tc, x, state, Wk, Wv, Wr, Wo, time_decay, time_cu
             contract(out_sums_of[n][:], (h_codes, h_scales, token_columns), (codes, scales, unit_columns))
 
         def store_out(n):
-            j = n - first_out_unit
-            out_sb = stores.tile([P, PAIR * P], F32)
+            first, count = store_of[n]
+            if n == first:
+                out_sb_of[first] = keep.tile([P, count * PAIR * P], F32, name="out_sb_%d" % first)
+            here = out_sb_of[first][:, (n - first) * PAIR * P : (n - first + 1) * PAIR * P]
             nc.scalar.copy(
-                out=out_sb[:].rearrange("k (c e) -> k c e", e=PAIR),
+                out=here.rearrange("k (c e) -> k c e", e=PAIR),
                 in_=out_sums_of[n][:].rearrange("k (e c) -> k c e", e=PAIR),
             )
-            nc.sync.dma_start(out=out_rows[:, j * PAIR * P : (j + 1) * PAIR * P], in_=out_sb[:])
+            if n == first + count - 1:
+                start = (first - first_out_unit) * PAIR * P
+                nc.sync.dma_start(out=out_rows[:, start : start + count * PAIR * P], in_=out_sb_of[first][:])
 
         def finish_on_scalar(i):
             w, g = steps[i]
@@ -306,19 +318,12 @@ def tile_rwkvtimemix_pa_kernel(tc, x, state, Wk, Wv, Wr, Wo, time_decay, time_cu
             bank = banks.tile([P, BANK], F32, tag="bank")
             for value in range(PACK):
                 nc.tensor.transpose(bank[:, value * P : (value + 1) * P], new_state_of[g][:, value, :], ident[:])
-            natural = stores.tile([P, BANK], F32)
             nc.scalar.copy(
-                out=natural[:].rearrange("k (u c e) -> k u c e", u=PAIR, e=PAIR),
+                out=new_state_sb[:, g * BANK : (g + 1) * BANK].rearrange("k (u c e) -> k u c e", u=PAIR, e=PAIR),
                 in_=bank[:].rearrange("k (u e c) -> k u c e", u=PAIR, e=PAIR),
             )
-            return natural
-
-        returned = []
-
-        def store_returned():
-            for g, natural in returned:
-                nc.sync.dma_start(out=new_state_rows[:, g * BANK : (g + 1) * BANK], in_=natural[:])
-            returned.clear()
+            if g == PASSES - 1:
+                nc.sync.dma_start(out=new_state_rows, in_=new_state_sb[:])
 
         for n in range(last_unit + 1):
             i, u = divmod(n, STEP_UNITS)
@@ -336,9 +341,7 @@ def tile_rwkvtimemix_pa_kernel(tc, x, state, Wk, Wv, Wr, Wo, time_decay, time_cu
                 else:
                     end_on_vector(finishing)
                     if steps[finishing][0] == RECEPTANCE:
-                        returned.append((steps[finishing][1], return_new_state(steps[finishing][1])))
-            if i + LOAD_AHEAD >= len(steps) - 1:
-                store_returned()
+                        return_new_state(steps[finishing][1])
             if 0 <= n - MULTIPLY_AFTER < first_out_unit:
                 multiply(n - MULTIPLY_AFTER)
             if n - MULTIPLY_OUT_AFTER >= first_out_unit:

from contextlib import ExitStack

import concourse.mybir as mybir
from concourse.masks import make_identity

F32 = mybir.dt.float32
BF16 = mybir.dt.bfloat16
U32 = mybir.dt.uint32
U8 = mybir.dt.uint8
FP8X4 = mybir.dt.float8_e4m3fn_x4
MULT = mybir.AluOpType.mult
ADD = mybir.AluOpType.add
SUB = mybir.AluOpType.subtract
ACT = mybir.ActivationFunctionType

P = 128
TOKENS = 128
SEQ_LEN = 32
CHANNELS = 2048
PACK = 4
PAIR = 2
PASSES = CHANNELS // (P * PACK)
UNITS = CHANNELS // (P * PAIR)
ROW_WORDS = CHANNELS // PAIR
BANK = 512
BANK_BLOCKS = BANK // P
CHUNK_BANKS = ROW_WORDS // BANK
STEP_UNITS = 2
RAW_BUFS = 6
LOAD_AHEAD = RAW_BUFS - 1
STATE_AFTER = 2
MULTIPLY_AFTER = 2
MULTIPLY_OUT_AFTER = 4
VECTOR_JOINS_AT = 2
KEY = 0
VALUE = 1
RECEPTANCE = 2
OUTPUT = 3

FLOPS = 4 * 2 * TOKENS * CHANNELS * CHANNELS


def tile_rwkvtimemix_pa_kernel(tc, x, state, Wk, Wv, Wr, Wo, time_decay, time_curve, out_0, out_1):
    nc = tc.nc
    weights = (Wk, Wv, Wr, Wo)
    out_rows = out_0.rearrange("b t d -> (b t) d")
    new_state_rows = out_1.rearrange("b t d -> (b t) d")

    steps = []
    for g in range(PASSES):
        steps.extend([(KEY, g), (VALUE, g), (RECEPTANCE, g)])
    for g in range(PASSES):
        steps.append((OUTPUT, g))
    first_out_unit = STEP_UNITS * steps.index((OUTPUT, 0))
    last_unit = STEP_UNITS * len(steps) - 1

    with ExitStack() as ctx:
        ctx.enter_context(tc.manual_schedule())
        keep = ctx.enter_context(tc.tile_pool(name="keep", bufs=1))
        raw_pool = ctx.enter_context(tc.tile_pool(name="raw", bufs=RAW_BUFS))
        grouped_pool = ctx.enter_context(tc.tile_pool(name="grouped", bufs=4))
        codes_pool = ctx.enter_context(tc.tile_pool(name="codes", bufs=MULTIPLY_OUT_AFTER + 1))
        work = ctx.enter_context(tc.tile_pool(name="work", bufs=2))
        banks = ctx.enter_context(tc.psum_pool(name="banks", bufs=6))
        sums = ctx.enter_context(tc.psum_pool(name="sums", bufs=2))

        x_sb = keep.tile([P, CHANNELS], BF16)
        nc.sync.dma_start(out=x_sb[:], in_=x.rearrange("b t d -> (b t) d"))
        vectors = keep.tile([P, P * PAIR], BF16)
        nc.vector.memset(vectors[:], 0.0)
        nc.sync.dma_start(out=vectors[0:UNITS, :], in_=time_curve.rearrange("(j c) -> j c", j=UNITS))
        nc.sync.dma_start(out=vectors[UNITS : 2 * UNITS, :], in_=time_decay.rearrange("(j c) -> j c", j=UNITS))

        ident = keep.tile([P, P], F32)
        make_identity(nc, ident[:])
        shift = keep.tile([P, P], F32)
        nc.vector.memset(shift[:], 0.0)
        nc.vector.tensor_copy(
            out=shift[:].rearrange("p (b t) -> p b t", t=SEQ_LEN)[:, :, 1:SEQ_LEN],
            in_=ident[:].rearrange("p (b t) -> p b t", t=SEQ_LEN)[:, :, 0 : SEQ_LEN - 1],
        )
        step = keep.tile([P, P], BF16)
        nc.vector.tensor_tensor(out=step[:], in0=ident[:], in1=shift[:], op=SUB)

        state_sb = keep.tile([P, CHANNELS], BF16)
        raw_words = {}

        def load_step(i):
            if i == STATE_AFTER:
                nc.sync.dma_start(out=state_sb[:], in_=state.rearrange("b t d -> (b t) d"))
            w, g = steps[i]
            raw = raw_pool.tile([P, STEP_UNITS, PAIR, CHANNELS], BF16)
            rows = weights[w][g * BANK : (g + 1) * BANK, :].rearrange("(u p e) k -> p u e k", u=STEP_UNITS, e=PAIR)
            if i < len(steps) - 2:
                halves = [slice(0, CHANNELS)]
            else:
                halves = [slice(0, CHANNELS // 2), slice(CHANNELS // 2, CHANNELS)]
            pieces = [(u, cols) for u in range(STEP_UNITS) for cols in halves]
            for u, cols in pieces:
                nc.sync.dma_start(out=raw[:, u, :, cols], in_=rows[:, u, :, cols])
            for u in range(STEP_UNITS):
                raw_words[STEP_UNITS * i + u] = raw[:, u, :, :].rearrange("p e k -> p (e k)").bitcast(F32)

        for i in range(LOAD_AHEAD):
            load_step(i)

        bank = banks.tile([P, BANK], F32, tag="bank")
        nc.tensor.transpose(bank[:, 0:P], vectors[:].bitcast(F32), ident[:])
        per_channel = keep.tile([P, 2 * UNITS * PAIR], F32)
        nc.vector.tensor_copy(out=per_channel[:], in_=bank[:].bitcast(BF16)[:, 0 : 2 * UNITS * PAIR])
        curve = per_channel[:, 0 : UNITS * PAIR]
        exp_decay = keep.tile([P, UNITS * PAIR], F32)
        nc.scalar.activation(out=exp_decay[:], in_=per_channel[:, UNITS * PAIR : 2 * UNITS * PAIR], func=ACT.Exp)
        decay = keep.tile([P, UNITS * PAIR], F32)
        nc.scalar.activation(out=decay[:], in_=exp_decay[:], func=ACT.Exp, scale=-1.0)
        table_loader = keep.tile([P, 1], F32)
        nc.scalar.activation(out=table_loader[:], in_=decay[:, 0:1], func=ACT.Sigmoid)

        x_words = x_sb[:].bitcast(F32)
        x_pairs = x_sb[:].rearrange("k (j c e) -> k j c e", j=UNITS, e=PAIR)
        xm_grouped = keep.tile([P, PASSES, TOKENS, PACK], BF16, align_bytes=64)
        for half in range(PASSES // PAIR):
            before = banks.tile([P, BANK], F32, tag="bank")
            for q in range(BANK_BLOCKS):
                j = half * BANK_BLOCKS + q
                nc.tensor.transpose(before[:, q * P : (q + 1) * P], x_words[:, j * P : (j + 1) * P], shift[:])
            before_pairs = before[:].bitcast(BF16).rearrange("p (g u k e) -> p g k u e", g=PAIR, u=PAIR, e=PAIR)
            for q in range(PAIR):
                g = half * PAIR + q
                change = sums.tile([P, BANK], F32, tag="sum")
                for u in range(PAIR):
                    for e in range(PAIR):
                        value = PAIR * u + e
                        nc.tensor.matmul(
                            out=change[:, value * P : (value + 1) * P],
                            lhsT=x_pairs[:, PAIR * g + u, :, e],
                            rhs=step[:],
                            start=True,
                            stop=True,
                        )
                scaled = work.tile([P, PACK, TOKENS], F32)
                nc.vector.tensor_tensor(
                    out=scaled[:],
                    in0=change[:].rearrange("p (t k) -> p t k", t=PACK),
                    in1=curve[:, PACK * g : PACK * (g + 1)].unsqueeze(2).to_broadcast([P, PACK, TOKENS]),
                    op=MULT,
                )
                nc.vector.tensor_tensor(
                    out=xm_grouped[:, g, :, :].rearrange("p k (u e) -> p k u e", e=PAIR),
                    in0=before_pairs[:, q, :, :, :],
                    in1=scaled[:].rearrange("p (u e) k -> p k u e", e=PAIR),
                    op=ADD,
                )
        xm_codes = keep.tile([P, PASSES * TOKENS], U32, align_bytes=64)
        xm_scales = keep.tile([P, PASSES * TOKENS], U8, align_bytes=64)
        nc.vector.quantize_mx(
            out=xm_codes[:].bitcast(FP8X4),
            scales=xm_scales[:],
            in_=xm_grouped[:].rearrange("p g k t -> p (g k t)"),
        )

        state_words = state_sb[:].bitcast(F32)

        h_codes = keep.tile([P, PASSES * TOKENS], U32, align_bytes=64)
        h_scales = keep.tile([P, PASSES * TOKENS], U8, align_bytes=64)

        grouped_of = {}
        quantised = {}
        sums_of = {}
        store_of = {}
        first = first_out_unit
        while first <= last_unit:
            count = max(1, (last_unit + 1 - first) // 2)
            for n in range(first, first + count):
                store_of[n] = (first, count)
            first += count
        out_sb_of = {}
        new_state_sb = keep.tile([P, CHANNELS], F32)
        out_sums_of = {}
        k_of = {}
        new_state_of = {}
        gate_of = {}
        h_of = {}

        def transpose(n):
            grouped = grouped_pool.tile([P, PASSES * PAIR * P * PACK], BF16, align_bytes=64)
            grouped_words = grouped[:].bitcast(F32).rearrange("p (g e c u) -> p g e c u", g=PASSES, e=PAIR, u=PAIR)
            for half in range(CHUNK_BANKS):
                for e in range(PAIR):
                    bank = banks.tile([P, BANK], F32, tag="bank")
                    for q in range(BANK_BLOCKS):
                        first = e * ROW_WORDS + half * BANK + q * P
                        nc.tensor.transpose(bank[:, q * P : (q + 1) * P], raw_words[n][:, first : first + P], ident[:])
                    source = bank[:].rearrange("p (g u c) -> p g c u", g=PAIR, u=PAIR)
                    target = grouped_words[:, PAIR * half : PAIR * half + PAIR, e, :, :]
                    if n >= VECTOR_JOINS_AT and half == CHUNK_BANKS - 1 and e == PAIR - 1:
                        nc.vector.tensor_copy(out=target, in_=source)
                    else:
                        nc.scalar.copy(out=target, in_=source)
            grouped_of[n] = grouped

        def quantise(n):
            codes = codes_pool.tile([P, PASSES * PAIR * P], U32, align_bytes=64)
            scales = codes_pool.tile([P, PASSES * PAIR * P], U8, align_bytes=64)
            for half in range(CHUNK_BANKS):
                cols = slice(half * PASSES * P, (half + 1) * PASSES * P)
                nc.vector.quantize_mx(
                    out=codes[:, cols].bitcast(FP8X4),
                    scales=scales[:, cols],
                    in_=grouped_of[n][:, half * PASSES * P * PACK : (half + 1) * PASSES * P * PACK],
                )
            quantised[n] = (codes, scales)

        def contract(target, stationary, moving):
            for g in range(PASSES):
                nc.tensor.matmul_mx(
                    out=target,
                    lhsT=stationary[0][:, stationary[2](g)].bitcast(FP8X4),
                    lhsT_scale=stationary[1][:, stationary[2](g)],
                    rhs=moving[0][:, moving[2](g)].bitcast(FP8X4),
                    rhs_scale=moving[1][:, moving[2](g)],
                    start=(g == 0),
                    stop=(g == PASSES - 1),
                )

        def token_columns(g):
            return slice(g * TOKENS, (g + 1) * TOKENS)

        def unit_columns(g):
            return slice(g * PAIR * P, (g + 1) * PAIR * P)

        def chunk_columns(e):
            return lambda g: slice((g * PAIR + e) * P, (g * PAIR + e + 1) * P)

        def multiply(n):
            i, u = divmod(n, STEP_UNITS)
            if u == 0:
                sums_of[i] = sums.tile([P, PACK, TOKENS], F32, tag="sum", name="products")
            codes, scales = quantised[n]
            for e in range(PAIR):
                contract(
                    sums_of[i][:, PAIR * u + e, :],
                    (codes, scales, chunk_columns(e)),
                    (xm_codes, xm_scales, token_columns),
                )

        def multiply_out(n):
            codes, scales = quantised[n]
            if n > last_unit - MULTIPLY_OUT_AFTER:
                out_sums_of[n] = banks.tile([P, PAIR * P], F32, tag="bank", name="out_sums")
            else:
                out_sums_of[n] = sums.tile([P, PAIR * P], F32, tag="sum", name="out_sums")
            contract(out_sums_of[n][:], (h_codes, h_scales, token_columns), (codes, scales, unit_columns))

        def store_out(n):
            first, count = store_of[n]
            if n == first:
                out_sb_of[first] = keep.tile([P, count * PAIR * P], F32, name="out_sb_%d" % first)
            here = out_sb_of[first][:, (n - first) * PAIR * P : (n - first + 1) * PAIR * P]
            nc.scalar.copy(
                out=here.rearrange("k (c e) -> k c e", e=PAIR),
                in_=out_sums_of[n][:].rearrange("k (e c) -> k c e", e=PAIR),
            )
            if n == first + count - 1:
                start = (first - first_out_unit) * PAIR * P
                nc.sync.dma_start(out=out_rows[:, start : start + count * PAIR * P], in_=out_sb_of[first][:])

        def finish_on_scalar(i):
            w, g = steps[i]
            if w == KEY:
                k_of[g] = work.tile([P, PACK, TOKENS], F32, name="k_sb")
                nc.scalar.copy(out=k_of[g][:], in_=sums_of[i][:])
            elif w == RECEPTANCE:
                gate_of[g] = work.tile([P, PACK, TOKENS], F32, name="gate")
                nc.scalar.activation(out=gate_of[g][:], in_=sums_of[i][:], func=ACT.Sigmoid)

        def begin_on_vector(i):
            w, g = steps[i]
            if w == VALUE:
                new_state_of[g] = work.tile([P, PACK, TOKENS], F32, name="new_state_t")
                nc.vector.tensor_tensor(out=new_state_of[g][:], in0=sums_of[i][:], in1=k_of[g][:], op=MULT)
            elif w == RECEPTANCE:
                h_of[g] = work.tile([P, TOKENS, PACK], BF16, align_bytes=64, name="h_grouped")
                nc.vector.tensor_tensor(
                    out=h_of[g][:],
                    in0=gate_of[g][:].rearrange("p t k -> p k t"),
                    in1=new_state_of[g][:].rearrange("p t k -> p k t"),
                    op=MULT,
                )

        def end_on_vector(i):
            w, g = steps[i]
            if w == VALUE:
                bank = banks.tile([P, BANK], F32, tag="bank")
                for u in range(PAIR):
                    j = PAIR * g + u
                    nc.tensor.transpose(bank[:, u * P : (u + 1) * P], state_words[:, j * P : (j + 1) * P], ident[:])
                state_pairs = bank[:].bitcast(BF16)[:, 0 : PAIR * TOKENS * PAIR].rearrange("p (u k e) -> p u k e", u=PAIR, e=PAIR)
                for u in range(PAIR):
                    for e in range(PAIR):
                        j = PAIR * g + u
                        nc.vector.scalar_tensor_tensor(
                            out=new_state_of[g][:, PAIR * u + e, :],
                            in0=state_pairs[:, u, :, e],
                            scalar=decay[:, PAIR * j + e : PAIR * j + e + 1],
                            in1=new_state_of[g][:, PAIR * u + e, :],
                            op0=MULT,
                            op1=ADD,
                        )
            elif w == RECEPTANCE:
                nc.vector.quantize_mx(
                    out=h_codes[:, token_columns(g)].bitcast(FP8X4),
                    scales=h_scales[:, token_columns(g)],
                    in_=h_of[g][:].rearrange("p k t -> p (k t)"),
                )

        def return_new_state(g):
            bank = banks.tile([P, BANK], F32, tag="bank")
            for value in range(PACK):
                nc.tensor.transpose(bank[:, value * P : (value + 1) * P], new_state_of[g][:, value, :], ident[:])
            nc.scalar.copy(
                out=new_state_sb[:, g * BANK : (g + 1) * BANK].rearrange("k (u c e) -> k u c e", u=PAIR, e=PAIR),
                in_=bank[:].rearrange("k (u e c) -> k u c e", u=PAIR, e=PAIR),
            )
            if g == PASSES - 1:
                nc.sync.dma_start(out=new_state_rows, in_=new_state_sb[:])

        for n in range(last_unit + 1):
            i, u = divmod(n, STEP_UNITS)
            if u == 0 and i + LOAD_AHEAD < len(steps):
                load_step(i + LOAD_AHEAD)
            finishing = i - STEP_UNITS if 0 <= STEP_UNITS * (i - STEP_UNITS) < first_out_unit else None
            if u == 0 and finishing is not None:
                finish_on_scalar(finishing)
            if n > 0:
                quantise(n - 1)
            transpose(n)
            if finishing is not None:
                if u == 0:
                    begin_on_vector(finishing)
                else:
                    end_on_vector(finishing)
                    if steps[finishing][0] == RECEPTANCE:
                        return_new_state(steps[finishing][1])
            if 0 <= n - MULTIPLY_AFTER < first_out_unit:
                multiply(n - MULTIPLY_AFTER)
            if n - MULTIPLY_OUT_AFTER >= first_out_unit:
                multiply_out(n - MULTIPLY_OUT_AFTER)
                store_out(n - MULTIPLY_OUT_AFTER)
        quantise(last_unit)
        for n in range(last_unit - MULTIPLY_OUT_AFTER + 1, last_unit + 1):
            multiply_out(n)
            store_out(n)
